import numpy as np
import ml_dtypes


def mxq(x, axis, fmt="e4m3"):
    dtype, down = {"e4m3": (ml_dtypes.float8_e4m3fn, 7), "e5m2": (ml_dtypes.float8_e5m2, 14)}[fmt]
    v = np.moveaxis(np.asarray(x, np.float32).astype(ml_dtypes.bfloat16).astype(np.float64), axis, -1)
    blocks = v.reshape(v.shape[:-1] + (-1, 32))
    amax = np.abs(blocks).max(-1, keepdims=True)
    byte = np.maximum(np.where(amax > 0, np.frexp(amax)[1] - 1 + 127, 0) - down, 1)
    scale = np.exp2(byte - 127.0)
    codes = (blocks / scale).astype(np.float32).astype(dtype).astype(np.float64)
    return np.moveaxis((codes * scale).reshape(v.shape), -1, axis)


WIDE = False


def mx_kscale(k):
    if not WIDE:
        return np.ones(k)
    levels = np.array([10, -10, 5, -5, 0])
    if k % 512:
        return np.exp2(np.random.permutation(np.resize(levels, k // 32))).repeat(32)
    a = np.empty((k // 512, 16))
    for p in range(k // 512):
        a[p, :8] = np.random.permutation(np.resize(levels, 8))
        for g in range(8):
            far = levels[np.abs(levels - a[p, g]) >= 10]
            a[p, g + 8] = far[np.random.randint(len(far))]
    return np.exp2(a.ravel()).repeat(32)


BF16 = ml_dtypes.bfloat16


def bf(x):
    return np.asarray(x, np.float32).astype(BF16)


def f64(x):
    return np.asarray(x).astype(np.float64)


B, C, P, NH, NW = 4, 4, 16, 16, 16
D = C * P * P
QK_SCALE = 1.0


def rel_bias(p):
    i = np.arange(p, dtype=np.float64)
    down = np.exp(-i / (p / 2))[:, None] * np.ones((1, p))
    right = down.T
    br = np.exp(-(i[:, None] + i[None, :]) / (p / 2))
    return np.stack([
        np.rot90(br, 2), np.flip(down, 0), np.rot90(br, 1),
        np.flip(right, 1), np.ones((p, p)), right,
        np.rot90(br, 3), down, br,
    ], axis=0)


def draw0():
    s = mx_kscale(D)
    sx = np.tile(s.reshape(C, P, P), (1, NH, NW))
    return {"x": bf(np.random.standard_normal((B, C, NH * P, NW * P)) * sx),
            "W_qkv": bf(np.random.standard_normal((3 * D, D)) / np.sqrt(D) / s),
            "b_qkv": bf(np.random.standard_normal(3 * D) * 0.5)}


def core(x, W_qkv, b_qkv):
    p, c = P, C
    b, _, h, w = x.shape
    nh, nw = h // p, w // p
    feat = f64(x).reshape(b, c, nh, p, nw, p).transpose(0, 2, 4, 1, 3, 5).reshape(b, nh, nw, c * p * p)
    y = mxq(feat, 3, "e4m3") @ mxq(f64(W_qkv), 1, "e4m3").T
    qkv = np.pad(y, ((0, 0), (1, 1), (1, 1), (0, 0))) + f64(b_qkv)
    qkv = qkv.reshape(b, nh + 2, nw + 2, 3, c, p, p)
    core_q = qkv[:, 1:nh + 1, 1:nw + 1, 0] * QK_SCALE
    k = np.stack([qkv[:, di:di + nh, dj:dj + nw, 1] for di in range(3) for dj in range(3)], axis=3)
    v = np.stack([qkv[:, di:di + nh, dj:dj + nw, 2] for di in range(3) for dj in range(3)], axis=3)
    bias = rel_bias(p)
    attn = core_q[:, :, :, None] * k * bias[:, None]
    out = np.sum(attn * v, axis=3)
    return out.transpose(0, 3, 1, 4, 2, 5).reshape(b, c, nh * p, nw * p)


def e4m3fn_bytes(y):
    return np.clip(np.asarray(y, np.float64), -448.0, 448.0).astype(np.float32).astype(ml_dtypes.float8_e4m3fn).view(np.uint8)


def e4m3fn_values(b):
    return np.asarray(b, np.uint8).view(ml_dtypes.float8_e4m3fn).astype(np.float64)


def setup_inputs():
    d = draw0()
    x0 = np.asarray(d['W_qkv']).astype(np.float64)
    s = (np.max(np.abs(x0), axis=(0,), keepdims=True) / 448.0).astype(np.float32)
    out = {}
    for k, v in d.items():
        if k == 'W_qkv':
            out['W_qkv_bytes'] = e4m3fn_bytes(x0 / s.astype(np.float64))
            out['W_qkv_scale'] = s
        else:
            out[k] = v
    return out


def reference(x, W_qkv_bytes, W_qkv_scale, b_qkv):
    return core(x, e4m3fn_values(W_qkv_bytes) * W_qkv_scale.astype(np.float64), b_qkv)

@@ -1,0 +1,548 @@
+from contextlib import ExitStack
+
+import concourse.mybir as mybir
+from concourse.masks import make_identity
+
+F32 = mybir.dt.float32
+BF16 = mybir.dt.bfloat16
+U8 = mybir.dt.uint8
+U32 = mybir.dt.uint32
+I32 = mybir.dt.int32
+FP8 = mybir.dt.float8_e4m3fn
+FP8X4 = mybir.dt.float8_e4m3fn_x4
+ALU = mybir.AluOpType
+ACT = mybir.ActivationFunctionType
+
+FLOPS = 2 * 1024 * 1024 * 3072
+
+P = 128
+NT = 8
+LATE = 4
+LATE_HALVES = (0, 1)
+UPPER_TS = False
+RING_POOL = False
+XR_V = 0
+QA = 3
+BIAS_FIRST = False
+NB_WHOLE = False
+WIDE_FROM = 2
+QLAST = False
+PAX = 1
+DEEP = True
+UB = 3
+KQB = 4
+TTB = 3
+HEAD = False
+GCONST = False
+TAIL_SPLIT = False
+QUANT_WIDE_FROM = 2
+
+
+def tile_attentionconv_kernel(tc, x, W_qkv_bytes, W_qkv_scale, b_qkv, out):
+    nc = tc.nc
+    with ExitStack() as ctx:
+        const = ctx.enter_context(tc.tile_pool(name="const", bufs=1))
+        xpool = ctx.enter_context(tc.tile_pool(name="xpool", bufs=1))
+        wkeep = ctx.enter_context(tc.tile_pool(name="wkeep", bufs=1))
+        wwork = ctx.enter_context(tc.tile_pool(name="wwork", bufs=3))
+        epi = ctx.enter_context(tc.tile_pool(name="epi", bufs=2))
+        ps = ctx.enter_context(tc.psum_pool(name="ps", bufs=2))
+        ctx.enter_context(tc.manual_schedule())
+
+        scale3 = const.tile([P, 3, 1024], F32, name="scale3", tag="scale3")
+        scale_bc = scale3[:, 0, :]
+        pidx = const.tile([P, 1], I32, name="pidx", tag="pidx")
+        nc.gpsimd.iota(pidx[:], pattern=[[0, 1]], base=0, channel_multiplier=1)
+        brow = const.tile([P, P], BF16, name="brow", tag="brow")
+        nc.gpsimd.memset(brow[:], 0.0)
+        b_rows = b_qkv.rearrange("(w m) -> w m", m=P)
+        s_row = W_qkv_scale.rearrange("o k -> (o k)")
+        if not BIAS_FIRST and not HEAD:
+            nc.scalar.dma_start(out=scale_bc, in_=W_qkv_scale.rearrange("o k -> (o k)").partition_broadcast(P))
+        nc.scalar.dma_start(out=brow[0:16, :], in_=b_rows[0:16, :])
+        nc.scalar.dma_start(out=brow[16:24, :], in_=b_rows[16:24, :])
+        if BIAS_FIRST and not HEAD:
+            nc.scalar.dma_start(out=scale_bc, in_=W_qkv_scale.rearrange("o k -> (o k)").partition_broadcast(P))
+
+        w_rows = W_qkv_bytes.rearrange("(w m) k -> m w k", m=P)
+        wbytes = {}
+
+        def load_w(t):
+            wb = wkeep.tile([P, 3, 1024], U8, name="wbytes%d" % t, tag="wbytes%d" % t)
+            if HEAD and t == 0:
+                for j in range(3):
+                    if j < 2:
+                        nc.sync.dma_start(out=scale3[:, 0, 512 * j : 512 * (j + 1)], in_=s_row[512 * j : 512 * (j + 1)].partition_broadcast(P))
+                    nc.sync.dma_start(out=wb[:, j, :], in_=w_rows[:, NT * j, :])
+            else:
+                nc.sync.dma_start(out=wb[:], in_=w_rows[:, t : 24 : NT, :])
+            wbytes[t] = wb
+
+        xin = {}
+
+        def load_x(ch):
+            xt = xpool.tile([P, 2048], BF16, name="xin%d" % ch, tag="xin%d" % ch)
+            for b in range(4):
+                src = x[b, ch].rearrange("(i r) (jh w) -> jh i r w", r=16, jh=2)
+                for jh in range(2):
+                    nc.sync.dma_start(
+                        out=xt[64 * jh + b : 64 * (jh + 1) : 4, :].rearrange("p (r w) -> p r w", r=16),
+                        in_=src[jh],
+                    )
+            xin[ch] = xt
+
+        for kind, idx in [("w", 0), ("x", 0), ("w", 1), ("x", 1), ("w", 2), ("x", 2), ("x", 3), ("w", 3), ("w", 4), ("w", 5), ("w", 6), ("w", 7)]:
+            if kind == "w":
+                load_w(idx)
+            else:
+                load_x(idx)
+
+        ident = const.tile([P, P], F32, name="ident", tag="ident")
+        make_identity(nc, ident[:])
+        identb = const.tile([P, P], BF16, name="identb", tag="identb")
+        make_identity(nc, identb[:])
+        zeros = const.tile([P, P], F32, name="zeros", tag="zeros")
+        nc.vector.memset(zeros[:], 0.0)
+
+        sr_i = const.tile([P, 2], I32, name="sr_i", tag="sr_i")
+        nc.vector.tensor_scalar(out=sr_i[:, 0:1], in0=pidx[:], scalar1=15, scalar2=None, op0=ALU.bitwise_and)
+        nc.vector.tensor_scalar(out=sr_i[:, 1:2], in0=pidx[:], scalar1=4, scalar2=None, op0=ALU.logical_shift_right)
+        sr_f = const.tile([P, 2], F32, name="sr_f", tag="sr_f")
+        nc.vector.tensor_copy(out=sr_f[:], in_=sr_i[:])
+        args = const.tile([P, 6], F32, name="args", tag="args")
+        for col, (src_col, mul, add) in enumerate(
+            [(0, 0.125, -1.875), (0, -0.125, 0.0), (1, 0.125, -1.875), (1, 0.125, -0.875), (1, -0.125, 0.0), (1, -0.125, -1.0)]
+        ):
+            nc.vector.tensor_scalar(
+                out=args[:, col : col + 1], in0=sr_f[:, src_col : src_col + 1],
+                scalar1=mul, scalar2=add, op0=ALU.mult, op1=ALU.add,
+            )
+        cf = const.tile([P, 6], F32, name="cf", tag="cf")
+        nc.scalar.activation(out=cf[:], in_=args[:], func=ACT.Exp)
+        if WIDE_FROM < NT:
+            nc.scalar.copy(out=scale3[:, 1, :], in_=scale_bc)
+            nc.scalar.copy(out=scale3[:, 2, :], in_=scale_bc)
+        c0 = cf[:, 0:1]
+        c2 = cf[:, 1:2]
+        csum = const.tile([P, 1], F32, name="csum", tag="csum")
+        if GCONST:
+            nc.gpsimd.tensor_tensor(out=csum[:], in0=c0, in1=c2, op=ALU.add)
+            nc.gpsimd.tensor_scalar(out=csum[:], in0=csum[:], scalar1=1.0, scalar2=None, op0=ALU.add)
+        elif not HEAD:
+            nc.vector.scalar_tensor_tensor(out=csum[:], in0=c0, scalar=1.0, in1=c2, op0=ALU.add, op1=ALU.add)
+
+        b_f = const.tile([P, 24], F32, name="b_f", tag="b_f")
+        bkbv = const.tile([P, NT], F32, name="bkbv", tag="bkbv")
+        tbord = const.tile([P, NT], F32, name="tbord", tag="tbord")
+        ub0 = const.tile([P, NT], F32, name="ub0", tag="ub0")
+        ub2 = const.tile([P, NT], F32, name="ub2", tag="ub2")
+
+        def bias_consts():
+            bps = ps.tile([P, P], BF16, name="bps", tag="ev", bufs=4)
+            nc.tensor.transpose(out=bps[:], in_=brow[:], identity=identb[:])
+            if HEAD and not GCONST:
+                nc.vector.scalar_tensor_tensor(out=csum[:], in0=c0, scalar=1.0, in1=c2, op0=ALU.add, op1=ALU.add)
+            if GCONST:
+                nc.scalar.copy(out=b_f[:], in_=bps[:, 0:24])
+            else:
+                nc.vector.tensor_copy(out=b_f[:], in_=bps[:, 0:24])
+            eng = nc.gpsimd if GCONST else nc.vector
+            eng.tensor_tensor(out=bkbv[:], in0=b_f[:, 8:16], in1=b_f[:, 16:24], op=ALU.mult)
+            eng.tensor_scalar(out=tbord[:], in0=bkbv[:], scalar1=csum[:], scalar2=None, op0=ALU.mult)
+            for rh in range(2):
+                eng.tensor_scalar(out=ub0[:, rh:NT:2], in0=tbord[:, rh:NT:2], scalar1=cf[:, 2 + rh : 3 + rh], scalar2=None, op0=ALU.mult)
+                eng.tensor_scalar(out=ub2[:, rh:NT:2], in0=tbord[:, rh:NT:2], scalar1=cf[:, 4 + rh : 5 + rh], scalar2=None, op0=ALU.mult)
+
+        wsc_of = {}
+        wg_of = {}
+        wq = {}
+        ws = {}
+
+        def w_scale(t):
+            wsc = wwork.tile([P, 3, 1024], BF16, name="wsc", tag="wsc", bufs=max(2, PAX))
+            if t >= WIDE_FROM:
+                nc.vector.tensor_tensor(
+                    out=wsc[:].rearrange("p j k -> p (j k)"), in0=wbytes[t][:].rearrange("p j k -> p (j k)").bitcast(FP8),
+                    in1=scale3[:].rearrange("p j k -> p (j k)"), op=ALU.mult,
+                )
+            for j in range(3):
+                if HEAD and t == 0 and j == 0:
+                    for h in range(2):
+                        ks = slice(512 * h, 512 * (h + 1))
+                        nc.vector.tensor_tensor(out=wsc[:, j, ks], in0=wbytes[t][:, j, ks].bitcast(FP8), in1=scale3[:, 0, ks], op=ALU.mult)
+                elif t < WIDE_FROM:
+                    nc.vector.tensor_tensor(out=wsc[:, j, :], in0=wbytes[t][:, j, :].bitcast(FP8), in1=scale_bc, op=ALU.mult)
+                wsc_of[(t, j)] = wsc[:, j, :]
+
+        def w_turn(t):
+            wg3 = wwork.tile([P, 3072], BF16, name="wg3", tag="wg", align_bytes=64, bufs=2)
+            for j in range(3):
+                words = wsc_of[(t, j)].bitcast(F32)
+                trp = ps.tile([P, 4, P], F32, name="trp", tag="ev", bufs=4)
+                for g in range(2):
+                    for u in range(2):
+                        nc.tensor.transpose(out=trp[:, 2 * g + u, :], in_=words[:, 256 * g + u : 256 * (g + 1) : 2], identity=ident[:])
+                wg = wg3[:, 1024 * j : 1024 * (j + 1)]
+                nc.scalar.copy(
+                    out=wg.bitcast(F32).rearrange("p (g m u) -> p g m u", g=2, u=2),
+                    in_=trp[:].rearrange("p (g u) m -> p g m u", g=2),
+                )
+            wg_of[t] = wg3
+
+        def w_quant(t):
+            wq_t = wkeep.tile([P, 768], U32, name="wq%d" % t, tag="wq%d" % t, align_bytes=64)
+            ws_t = wkeep.tile([P, 768], U8, name="ws%d" % t, tag="ws%d" % t, align_bytes=64)
+            for c0w, c1w in ([(0, 512), (512, 768)] if t >= QUANT_WIDE_FROM else [(0, 256), (256, 512), (512, 768)]):
+                nc.vector.quantize_mx(
+                    out=wq_t[:, c0w:c1w].bitcast(FP8X4),
+                    scales=ws_t[:, c0w:c1w],
+                    in_=wg_of[t][:, 4 * c0w : 4 * c1w],
+                )
+            wq[t] = wq_t
+            ws[t] = ws_t
+
+        xr_of = {}
+        xg_of = {}
+        xq = {}
+        xs = {}
+
+        def x_reorder(g):
+            xr = xpool.tile([P, 2048], F32, name="xr%d" % g, tag="xr%d" % g)
+            xr_v = xr[:].rearrange("p (jl u c2 r s4) -> p u c2 jl r s4", jl=8, u=2, c2=2, r=16)
+            for c2i in range(2):
+                xw = xin[2 * g + c2i][:].bitcast(F32).rearrange("p (r jl s4 u) -> p u jl r s4", r=16, jl=8, s4=4)
+                for u in range(2):
+                    if 2 * c2i + u < XR_V:
+                        nc.vector.tensor_copy(out=xr_v[:, u, c2i], in_=xw[:, u])
+                    else:
+                        nc.scalar.copy(out=xr_v[:, u, c2i], in_=xw[:, u])
+            xr_of[g] = xr
+
+        def x_turn(g):
+            xr = xr_of[g]
+            xg = xpool.tile([P, 4096], BF16, name="xg%d" % g, tag="xg%d" % g, align_bytes=64)
+            xg_v = xg[:].bitcast(F32).rearrange("p (jl m u) -> p jl m u", jl=8, u=2)
+            for a in range(4):
+                trp = ps.tile([P, 4, P], F32, name="trp", tag="ev", bufs=4)
+                for q4 in range(4):
+                    nc.tensor.transpose(out=trp[:, q4, :], in_=xr[:, (4 * a + q4) * P : (4 * a + q4 + 1) * P], identity=ident[:])
+                nc.scalar.copy(out=xg_v[:, 2 * a : 2 * a + 2], in_=trp[:].rearrange("p (jl u) m -> p jl m u", u=2))
+            xg_of[g] = xg
+            xq[g] = xpool.tile([P, 1024], U32, name="xq%d" % g, tag="xq%d" % g, align_bytes=64)
+            xs[g] = xpool.tile([P, 1024], U8, name="xs%d" % g, tag="xs%d" % g, align_bytes=64)
+
+        def x_quant(g, n):
+            nc.vector.quantize_mx(
+                out=xq[g][:, 512 * n : 512 * (n + 1)].bitcast(FP8X4),
+                scales=xs[g][:, 512 * n : 512 * (n + 1)],
+                in_=xg_of[g][:, 2048 * n : 2048 * (n + 1)],
+            )
+
+        def project(t, j, n, tag):
+            acc = ps.tile([P, 512], F32, name="acc_" + tag, tag=tag, bufs=(4 if tag == "ev" else 2))
+            for g in range(2):
+                cols = slice(256 * j + P * g, 256 * j + P * (g + 1))
+                nc.tensor.matmul_mx(
+                    out=acc[:],
+                    lhsT=wq[t][:, cols].bitcast(FP8X4),
+                    lhsT_scale=ws[t][:, cols],
+                    rhs=xq[g][:, 512 * n : 512 * (n + 1)].bitcast(FP8X4),
+                    rhs_scale=xs[g][:, 512 * n : 512 * (n + 1)],
+                    start=(g == 0),
+                    stop=(g == 1),
+                )
+            return acc
+
+        kvp_of = {}
+        u0_of = {}
+        u2_of = {}
+        kp_of = {}
+        vacc_of = {}
+        qacc_of = {}
+        qp_of = {}
+        qts_of = {}
+        tmp_of = {}
+        tt_of = {}
+        stp_of = {}
+        ot_of = {}
+        zb = zeros[:, 0:64].rearrange("p (a c) -> p a c", c=4)
+
+        def v_halves(t):
+            return LATE_HALVES if t >= LATE and not UPPER_TS else ()
+
+        def fill(dst, src, col):
+            if RING_POOL:
+                nc.gpsimd.tensor_scalar(out=dst, in0=src, scalar1=1.0, scalar2=col, op0=ALU.mult, op1=ALU.add)
+            else:
+                nc.scalar.activation(out=dst, in_=src, func=ACT.Identity, bias=col, scale=1.0)
+
+        def ring(t):
+            kvp = epi.tile([P, 1152], F32, name="kvp", tag="kvp")
+            fill(kvp[:].rearrange("p (k c) -> p k c", c=64)[:, 0:18:17, :], zeros[:].rearrange("p (a c) -> p a c", c=64), bkbv[:, t : t + 1])
+            kvp_of[t] = kvp
+            u2 = epi.tile([P, 16, 64], F32, name="u2", tag="u2", bufs=UB)
+            fill(u2[:, :, 60:64], zb, ub2[:, t : t + 1])
+            u2_of[t] = u2
+            u0 = epi.tile([P, 16, 64], F32, name="u0", tag="u0", bufs=UB)
+            u0_of[t] = u0
+            if len(v_halves(t)) == 0:
+                fill(u0[:, :, 0:4], zb, ub0[:, t : t + 1])
+            else:
+                for n in range(2):
+                    if n not in v_halves(t):
+                        fill(u0[:, 8 * n : 8 * (n + 1), 0:4], zeros[:, 0:32].rearrange("p (a c) -> p a c", c=4), ub0[:, t : t + 1])
+
+        def mx_kv(t):
+            for n in range(2):
+                kacc = project(t, 1, n, "ev")
+                vacc_of[(t, n)] = project(t, 2, n, "v")
+                kp = epi.tile([P, 512], F32, name="kp", tag="kp", bufs=KQB)
+                nc.scalar.activation(out=kp[:], in_=kacc[:], func=ACT.Identity, bias=b_f[:, 8 + t : 9 + t], scale=1.0)
+                kp_of[(t, n)] = kp
+
+        def mx_q(t):
+            for n in range(2):
+                qacc_of[(t, n)] = project(t, 0, n, "ev")
+
+        def q_bias(t):
+            for n in range(2):
+                qp = epi.tile([P, 512], F32, name="qp", tag="qp", bufs=KQB)
+                nc.scalar.activation(out=qp[:], in_=qacc_of[(t, n)][:], func=ACT.Identity, bias=b_f[:, t : t + 1], scale=1.0)
+                qp_of[(t, n)] = qp
+
+        def kv_mul(t):
+            for n in range(2):
+                nc.vector.scalar_tensor_tensor(
+                    out=kvp_of[t][:, 64 + 512 * n : 64 + 512 * (n + 1)], in0=vacc_of[(t, n)][:], scalar=b_f[:, 16 + t : 17 + t],
+                    in1=kp_of[(t, n)][:], op0=ALU.add, op1=ALU.mult,
+                )
+
+        def q_turn(t):
+            for n in range(2):
+                qtp = ps.tile([P, 4, P], F32, name="qtp", tag="ev", bufs=4)
+                for q4 in range(4):
+                    nc.tensor.transpose(out=qtp[:, q4, :], in_=qp_of[(t, n)][:, P * q4 : P * (q4 + 1)], identity=ident[:])
+                qts = epi.tile([P, 512], F32, name="qts", tag="qts", bufs=4)
+                nc.scalar.copy(out=qts[:], in_=qtp[:].rearrange("p jl e -> p (jl e)"))
+                qts_of[(t, n)] = qts
+
+        def h1(t):
+            kvp = kvp_of[t]
+            kvb = kvp[:].rearrange("p (k c) -> p k c", c=64)
+            tmp = epi.tile([P, 1024], F32, name="tmp", tag="tmp", bufs=1)
+            nc.vector.scalar_tensor_tensor(out=tmp[:, 128:1024], in0=kvp[:, 64:960], scalar=c0, in1=kvp[:, 192:1088], op0=ALU.mult, op1=ALU.add)
+            nc.vector.scalar_tensor_tensor(
+                out=tmp[:, 0:128].rearrange("p (k c) -> p k c", c=64), in0=kvb[:, 0:16:15, :], scalar=c0, in1=kvb[:, 1:3, :],
+                op0=ALU.mult, op1=ALU.add,
+            )
+            tmp_of[t] = tmp
+
+        def h2(t):
+            kvp = kvp_of[t]
+            kvb = kvp[:].rearrange("p (k c) -> p k c", c=64)
+            tmp = tmp_of[t]
+            tt = epi.tile([P, 1024], F32, name="tt", tag="tt", bufs=TTB)
+            nc.vector.scalar_tensor_tensor(out=tt[:, 0:896], in0=kvp[:, 192:1088], scalar=c2, in1=tmp[:, 0:896], op0=ALU.mult, op1=ALU.add)
+            nc.vector.scalar_tensor_tensor(
+                out=tt[:, 896:1024].rearrange("p (k c) -> p k c", c=64), in0=kvb[:, 2:18:15, :], scalar=c2,
+                in1=tmp[:, 896:1024].rearrange("p (k c) -> p k c", c=64), op0=ALU.mult, op1=ALU.add,
+            )
+            tt_of[t] = tt
+
+        def upper_tap(t):
+            rh = t % 2
+            tv = tt_of[t][:].rearrange("p (k c) -> p k c", c=64)
+            if UPPER_TS:
+                nc.vector.tensor_scalar(out=u0_of[t][:, :, 4:64], in0=tv[:, :, 0:60], scalar1=cf[:, 2 + rh : 3 + rh], scalar2=None, op0=ALU.mult)
+                return
+            yy = u0_of[t]
+            for ks in ([slice(0, 16)] if len(v_halves(t)) == 2 else [slice(8 * n, 8 * (n + 1)) for n in v_halves(t)]):
+                nc.vector.scalar_tensor_tensor(
+                    out=yy[:, ks, 4:64], in0=tv[:, ks, 0:60], scalar=cf[:, 2 + rh : 3 + rh], in1=tv[:, ks, 4:64], op0=ALU.mult, op1=ALU.add,
+                )
+                nc.vector.tensor_scalar(out=yy[:, ks, 0:4], in0=tv[:, ks, 0:4], scalar1=ub0[:, t : t + 1], scalar2=None, op0=ALU.add)
+
+        def neighbours(t):
+            rh = t % 2
+            tv = tt_of[t][:].rearrange("p (k c) -> p k c", c=64)
+            halves = [slice(8 * n, 8 * (n + 1)) for n in range(2)]
+            up = [halves[n] for n in range(2) if n not in v_halves(t) and not (UPPER_TS and t >= LATE)]
+            down = halves
+            if NB_WHOLE:
+                down = [slice(0, 16)]
+                if len(up) == 2:
+                    up = [slice(0, 16)]
+            for ks in down:
+                for ku in up:
+                    if ku.start == ks.start or (NB_WHOLE and ks.start == 0):
+                        nc.scalar.activation(out=u0_of[t][:, ku, 4:64], in_=tv[:, ku, 0:60], func=ACT.Copy, scale=cf[:, 2 + rh : 3 + rh])
+                nc.scalar.activation(out=u2_of[t][:, ks, 0:60], in_=tv[:, ks, 4:64], func=ACT.Copy, scale=cf[:, 4 + rh : 5 + rh])
+
+        def vertical(t):
+            u0 = u0_of[t][:].rearrange("p k c -> p (k c)")
+            u2 = u2_of[t][:].rearrange("p k c -> p (k c)")
+            for n in range(2):
+                stp = ps.tile([P, 4, P], F32, name="stp", tag="sT", bufs=2)
+                for q4 in range(4):
+                    cols = slice(P * (4 * n + q4), P * (4 * n + q4 + 1))
+                    three = n not in v_halves(t)
+                    if three:
+                        nc.tensor.matmul(out=stp[:, q4, :], lhsT=tt_of[t][:, cols], rhs=ident[:], start=True, stop=False, is_transpose=True)
+                    nc.tensor.matmul(out=stp[:, q4, :], lhsT=u0[:, cols], rhs=ident[:], start=(not three), stop=False, is_transpose=True)
+                    nc.tensor.matmul(out=stp[:, q4, :], lhsT=u2[:, cols], rhs=ident[:], start=False, stop=True, is_transpose=True)
+                stp_of[(t, n)] = stp
+
+        def fin(t, n):
+            if n == 0:
+                ot_of[t] = epi.tile([P, 1024], F32, name="ot", tag="ot", bufs=3)
+            ot_v = ot_of[t][:].rearrange("p (r jl s) -> p jl r s", r=8, jl=8)
+            nc.vector.tensor_tensor(
+                out=ot_v[:, 4 * n : 4 * (n + 1)],
+                in0=stp_of[(t, n)][:].rearrange("p jl (r s) -> p jl r s", s=16),
+                in1=qts_of[(t, n)][:].rearrange("p (jl r s) -> p jl r s", jl=4, s=16),
+                op=ALU.mult,
+            )
+
+        def stores(t, w0=0, w1=128):
+            ch, rh = divmod(t, 2)
+            for b in range(4):
+                dst = out[b, ch].rearrange("(i r) (jh w) -> jh i r w", r=16, jh=2)
+                for jh in range(2):
+                    nc.sync.dma_start(
+                        out=dst[jh, :, 8 * rh : 8 * (rh + 1), w0:w1],
+                        in_=ot_of[t][64 * jh + b : 64 * (jh + 1) : 4, :].rearrange("p (r w) -> p r w", r=8)[:, :, w0:w1],
+                    )
+
+        def ok(t):
+            return 0 <= t < NT
+
+        if QA == 4:
+            w_scale(0)
+            bias_consts()
+            w_turn(0)
+            w_scale(1)
+            w_quant(0)
+            x_reorder(0)
+            w_turn(1)
+            w_scale(2)
+            w_quant(1)
+            x_turn(0)
+            x_quant(0, 0)
+            x_quant(0, 1)
+            w_turn(2)
+            w_scale(3)
+            w_quant(2)
+            x_reorder(1)
+            x_turn(1)
+            w_turn(3)
+            w_scale(4)
+            x_quant(1, 0)
+            x_quant(1, 1)
+            w_quant(3)
+        elif QA == 3:
+            w_scale(0)
+            bias_consts()
+            w_turn(0)
+            w_scale(1)
+            w_quant(0)
+            x_reorder(0)
+            w_turn(1)
+            w_scale(2)
+            w_quant(1)
+            x_turn(0)
+            x_quant(0, 0)
+            x_quant(0, 1)
+            w_scale(3)
+            x_reorder(1)
+            x_turn(1)
+            if PAX >= 2:
+                w_scale(4)
+            x_quant(1, 0)
+            x_quant(1, 1)
+            w_turn(2)
+            w_quant(2)
+        else:
+            if BIAS_FIRST:
+                bias_consts()
+            w_scale(0)
+            if not BIAS_FIRST:
+                bias_consts()
+            w_turn(0)
+            x_reorder(0)
+            w_scale(1)
+            w_quant(0)
+            x_turn(0)
+            x_reorder(1)
+            w_turn(1)
+            x_quant(0, 0)
+            x_quant(0, 1)
+            x_turn(1)
+            w_scale(2)
+            w_quant(1)
+            x_quant(1, 0)
+            x_quant(1, 1)
+        ring(0)
+        mx_kv(0)
+        if PAX >= 3:
+            w_scale(QA + 2)
+        if not DEEP:
+            mx_q(0)
+            q_bias(0)
+
+        def last_stores(t, n):
+            if TAIL_SPLIT and t == NT - 1:
+                stores(t, 64 * n, 64 * (n + 1))
+            elif n == 1:
+                stores(t)
+
+        FD = 2 if DEEP else 1
+        for it in range(0, NT + 1 + (1 if DEEP else 0)):
+            if ok(it + QA):
+                w_turn(it + QA)
+            if ok(it):
+                kv_mul(it)
+            if ok(it - FD):
+                fin(it - FD, 0)
+                last_stores(it - FD, 0)
+            if ok(it - FD + 1) and not (QLAST and it - FD + 1 == NT - 1):
+                q_turn(it - FD + 1)
+            if ok(it):
+                h1(it)
+            if ok(it - FD):
+                fin(it - FD, 1)
+                last_stores(it - FD, 1)
+            if ok(it):
+                h2(it)
+                if it >= LATE:
+                    upper_tap(it)
+            if ok(it + 1):
+                mx_kv(it + 1)
+            if ok(it - FD + 2) and not (QLAST and it - FD + 2 == NT - 1):
+                mx_q(it - FD + 2)
+            if QLAST and it == NT - 2:
+                mx_q(NT - 1)
+            if DEEP:
+                if ok(it) and not (QLAST and it == NT - 1):
+                    q_bias(it)
+                if QLAST and it == NT - 2:
+                    q_bias(NT - 1)
+                if QLAST and it == NT - 1:
+                    q_turn(NT - 1)
+                if ok(it - 1):
+                    vertical(it - 1)
+                if ok(it):
+                    neighbours(it)
+                if ok(it + 1):
+                    ring(it + 1)
+            else:
+                if ok(it):
+                    neighbours(it)
+                if ok(it + 1):
+                    q_bias(it + 1)
+                    ring(it + 1)
+                if ok(it):
+                    vertical(it)
+            if ok(it + QA + PAX):
+                w_scale(it + QA + PAX)
+            if ok(it + QA):
+                w_quant(it + QA)

@@ -23,17 +23,13 @@ UPPER_TS = False
 RING_POOL = False
 XR_V = 0
 QA = 3
-BIAS_FIRST = False
 NB_WHOLE = False
-WIDE_FROM = 2
 QLAST = False
 PAX = 1
 DEEP = True
 UB = 3
 KQB = 4
 TTB = 3
-HEAD = False
-GCONST = False
 TAIL_SPLIT = False
 QUANT_WIDE_FROM = 2
 
@@ -49,33 +45,21 @@ def tile_attentionconv_kernel(tc, x, W_qkv_bytes, W_qkv_scale, b_qkv, out):
         ps = ctx.enter_context(tc.psum_pool(name="ps", bufs=2))
         ctx.enter_context(tc.manual_schedule())
 
-        scale3 = const.tile([P, 3, 1024], F32, name="scale3", tag="scale3")
-        scale_bc = scale3[:, 0, :]
         pidx = const.tile([P, 1], I32, name="pidx", tag="pidx")
         nc.gpsimd.iota(pidx[:], pattern=[[0, 1]], base=0, channel_multiplier=1)
+        srow = const.tile([P, P], F32, name="srow", tag="srow")
+        nc.vector.memset(srow[:], 0.0)
         brow = const.tile([P, P], BF16, name="brow", tag="brow")
         nc.gpsimd.memset(brow[:], 0.0)
         b_rows = b_qkv.rearrange("(w m) -> w m", m=P)
-        s_row = W_qkv_scale.rearrange("o k -> (o k)")
-        if not BIAS_FIRST and not HEAD:
-            nc.scalar.dma_start(out=scale_bc, in_=W_qkv_scale.rearrange("o k -> (o k)").partition_broadcast(P))
-        nc.scalar.dma_start(out=brow[0:16, :], in_=b_rows[0:16, :])
-        nc.scalar.dma_start(out=brow[16:24, :], in_=b_rows[16:24, :])
-        if BIAS_FIRST and not HEAD:
-            nc.scalar.dma_start(out=scale_bc, in_=W_qkv_scale.rearrange("o k -> (o k)").partition_broadcast(P))
+        nc.sync.dma_start(out=srow[0:8, :], in_=W_qkv_scale.rearrange("o (m n) -> (o m) n", n=P))
 
         w_rows = W_qkv_bytes.rearrange("(w m) k -> m w k", m=P)
         wbytes = {}
 
         def load_w(t):
             wb = wkeep.tile([P, 3, 1024], U8, name="wbytes%d" % t, tag="wbytes%d" % t)
-            if HEAD and t == 0:
-                for j in range(3):
-                    if j < 2:
-                        nc.sync.dma_start(out=scale3[:, 0, 512 * j : 512 * (j + 1)], in_=s_row[512 * j : 512 * (j + 1)].partition_broadcast(P))
-                    nc.sync.dma_start(out=wb[:, j, :], in_=w_rows[:, NT * j, :])
-            else:
-                nc.sync.dma_start(out=wb[:], in_=w_rows[:, t : 24 : NT, :])
+            nc.sync.dma_start(out=wb[:], in_=w_rows[:, t : 24 : NT, :])
             wbytes[t] = wb
 
         xin = {}
@@ -91,11 +75,14 @@ def tile_attentionconv_kernel(tc, x, W_qkv_bytes, W_qkv_scale, b_qkv, out):
                     )
             xin[ch] = xt
 
-        for kind, idx in [("w", 0), ("x", 0), ("w", 1), ("x", 1), ("w", 2), ("x", 2), ("x", 3), ("w", 3), ("w", 4), ("w", 5), ("w", 6), ("w", 7)]:
+        for kind, idx in [("w", 0), ("x", 0), ("b", 0), ("w", 1), ("x", 1), ("w", 2), ("x", 2), ("x", 3), ("w", 3), ("w", 4), ("w", 5), ("w", 6), ("w", 7)]:
             if kind == "w":
                 load_w(idx)
-            else:
+            elif kind == "x":
                 load_x(idx)
+            else:
+                nc.sync.dma_start(out=brow[0:16, :], in_=b_rows[0:16, :])
+                nc.sync.dma_start(out=brow[16:24, :], in_=b_rows[16:24, :])
 
         ident = const.tile([P, P], F32, name="ident", tag="ident")
         make_identity(nc, ident[:])
@@ -119,17 +106,25 @@ def tile_attentionconv_kernel(tc, x, W_qkv_bytes, W_qkv_scale, b_qkv, out):
             )
         cf = const.tile([P, 6], F32, name="cf", tag="cf")
         nc.scalar.activation(out=cf[:], in_=args[:], func=ACT.Exp)
-        if WIDE_FROM < NT:
-            nc.scalar.copy(out=scale3[:, 1, :], in_=scale_bc)
-            nc.scalar.copy(out=scale3[:, 2, :], in_=scale_bc)
         c0 = cf[:, 0:1]
         c2 = cf[:, 1:2]
         csum = const.tile([P, 1], F32, name="csum", tag="csum")
-        if GCONST:
-            nc.gpsimd.tensor_tensor(out=csum[:], in0=c0, in1=c2, op=ALU.add)
-            nc.gpsimd.tensor_scalar(out=csum[:], in0=csum[:], scalar1=1.0, scalar2=None, op0=ALU.add)
-        elif not HEAD:
-            nc.vector.scalar_tensor_tensor(out=csum[:], in0=c0, scalar=1.0, in1=c2, op0=ALU.add, op1=ALU.add)
+        nc.vector.scalar_tensor_tensor(out=csum[:], in0=c0, scalar=1.0, in1=c2, op0=ALU.add, op1=ALU.add)
+
+        scale_bc = const.tile([P, 1024], F32, name="scale_bc", tag="scale_bc")
+        scol = const.tile([P, 8], F32, name="scol", tag="scol")
+        sps = ps.tile([P, P], F32, name="sps", tag="ev", bufs=4)
+        nc.tensor.transpose(out=sps[:], in_=srow[:], identity=ident[:])
+        nc.vector.tensor_copy(out=scol[:], in_=sps[:, 0:8])
+        for h in range(2):
+            spb = ps.tile([P, 4, P], F32, name="spb", tag="ev", bufs=4)
+            for q4 in range(4):
+                m = 4 * h + q4
+                nc.tensor.transpose(out=spb[:, q4, :], in_=scol[:, m : m + 1].to_broadcast([P, P]), identity=ident[:])
+            if h == 0:
+                nc.vector.tensor_copy(out=scale_bc[:, 0:512], in_=spb[:].rearrange("p q n -> p (q n)"))
+            else:
+                nc.scalar.copy(out=scale_bc[:, 512:1024], in_=spb[:].rearrange("p q n -> p (q n)"))
 
         b_f = const.tile([P, 24], F32, name="b_f", tag="b_f")
         bkbv = const.tile([P, NT], F32, name="bkbv", tag="bkbv")
@@ -140,13 +135,8 @@ def tile_attentionconv_kernel(tc, x, W_qkv_bytes, W_qkv_scale, b_qkv, out):
         def bias_consts():
             bps = ps.tile([P, P], BF16, name="bps", tag="ev", bufs=4)
             nc.tensor.transpose(out=bps[:], in_=brow[:], identity=identb[:])
-            if HEAD and not GCONST:
-                nc.vector.scalar_tensor_tensor(out=csum[:], in0=c0, scalar=1.0, in1=c2, op0=ALU.add, op1=ALU.add)
-            if GCONST:
-                nc.scalar.copy(out=b_f[:], in_=bps[:, 0:24])
-            else:
-                nc.vector.tensor_copy(out=b_f[:], in_=bps[:, 0:24])
-            eng = nc.gpsimd if GCONST else nc.vector
+            nc.vector.tensor_copy(out=b_f[:], in_=bps[:, 0:24])
+            eng = nc.vector
             eng.tensor_tensor(out=bkbv[:], in0=b_f[:, 8:16], in1=b_f[:, 16:24], op=ALU.mult)
             eng.tensor_scalar(out=tbord[:], in0=bkbv[:], scalar1=csum[:], scalar2=None, op0=ALU.mult)
             for rh in range(2):
@@ -160,23 +150,16 @@ def tile_attentionconv_kernel(tc, x, W_qkv_bytes, W_qkv_scale, b_qkv, out):
 
         def w_scale(t):
             wsc = wwork.tile([P, 3, 1024], BF16, name="wsc", tag="wsc", bufs=max(2, PAX))
-            if t >= WIDE_FROM:
-                nc.vector.tensor_tensor(
-                    out=wsc[:].rearrange("p j k -> p (j k)"), in0=wbytes[t][:].rearrange("p j k -> p (j k)").bitcast(FP8),
-                    in1=scale3[:].rearrange("p j k -> p (j k)"), op=ALU.mult,
-                )
             for j in range(3):
-                if HEAD and t == 0 and j == 0:
-                    for h in range(2):
-                        ks = slice(512 * h, 512 * (h + 1))
-                        nc.vector.tensor_tensor(out=wsc[:, j, ks], in0=wbytes[t][:, j, ks].bitcast(FP8), in1=scale3[:, 0, ks], op=ALU.mult)
-                elif t < WIDE_FROM:
-                    nc.vector.tensor_tensor(out=wsc[:, j, :], in0=wbytes[t][:, j, :].bitcast(FP8), in1=scale_bc, op=ALU.mult)
+                for ks in [slice(0, 512), slice(512, 1024)] if t == 0 and j == 0 else [slice(0, 1024)]:
+                    nc.vector.tensor_tensor(out=wsc[:, j, ks], in0=wbytes[t][:, j, ks].bitcast(FP8), in1=scale_bc[:, ks], op=ALU.mult)
                 wsc_of[(t, j)] = wsc[:, j, :]
 
-        def w_turn(t):
-            wg3 = wwork.tile([P, 3072], BF16, name="wg3", tag="wg", align_bytes=64, bufs=2)
-            for j in range(3):
+        def w_turn(t, js=(0, 1, 2)):
+            if t not in wg_of:
+                wg_of[t] = wwork.tile([P, 3072], BF16, name="wg3", tag="wg", align_bytes=64, bufs=2)
+            wg3 = wg_of[t]
+            for j in js:
                 words = wsc_of[(t, j)].bitcast(F32)
                 trp = ps.tile([P, 4, P], F32, name="trp", tag="ev", bufs=4)
                 for g in range(2):
@@ -187,8 +170,6 @@ def tile_attentionconv_kernel(tc, x, W_qkv_bytes, W_qkv_scale, b_qkv, out):
                     out=wg.bitcast(F32).rearrange("p (g m u) -> p g m u", g=2, u=2),
                     in_=trp[:].rearrange("p (g u) m -> p g m u", g=2),
                 )
-            wg_of[t] = wg3
-
         def w_quant(t):
             wq_t = wkeep.tile([P, 768], U32, name="wq%d" % t, tag="wq%d" % t, align_bytes=64)
             ws_t = wkeep.tile([P, 768], U8, name="ws%d" % t, tag="ws%d" % t, align_bytes=64)
@@ -206,30 +187,31 @@ def tile_attentionconv_kernel(tc, x, W_qkv_bytes, W_qkv_scale, b_qkv, out):
         xq = {}
         xs = {}
 
-        def x_reorder(g):
-            xr = xpool.tile([P, 2048], F32, name="xr%d" % g, tag="xr%d" % g)
+        def x_reorder(g, cs=(0, 1)):
+            if g not in xr_of:
+                xr_of[g] = xpool.tile([P, 2048], F32, name="xr%d" % g, tag="xr%d" % g)
+            xr = xr_of[g]
             xr_v = xr[:].rearrange("p (jl u c2 r s4) -> p u c2 jl r s4", jl=8, u=2, c2=2, r=16)
-            for c2i in range(2):
+            for c2i in cs:
                 xw = xin[2 * g + c2i][:].bitcast(F32).rearrange("p (r jl s4 u) -> p u jl r s4", r=16, jl=8, s4=4)
                 for u in range(2):
                     if 2 * c2i + u < XR_V:
                         nc.vector.tensor_copy(out=xr_v[:, u, c2i], in_=xw[:, u])
                     else:
                         nc.scalar.copy(out=xr_v[:, u, c2i], in_=xw[:, u])
-            xr_of[g] = xr
-
-        def x_turn(g):
+        def x_turn(g, part=(0, 1, 2, 3)):
             xr = xr_of[g]
-            xg = xpool.tile([P, 4096], BF16, name="xg%d" % g, tag="xg%d" % g, align_bytes=64)
+            if g not in xg_of:
+                xg_of[g] = xpool.tile([P, 4096], BF16, name="xg%d" % g, tag="xg%d" % g, align_bytes=64)
+                xq[g] = xpool.tile([P, 1024], U32, name="xq%d" % g, tag="xq%d" % g, align_bytes=64)
+                xs[g] = xpool.tile([P, 1024], U8, name="xs%d" % g, tag="xs%d" % g, align_bytes=64)
+            xg = xg_of[g]
             xg_v = xg[:].bitcast(F32).rearrange("p (jl m u) -> p jl m u", jl=8, u=2)
-            for a in range(4):
+            for a in part:
                 trp = ps.tile([P, 4, P], F32, name="trp", tag="ev", bufs=4)
                 for q4 in range(4):
                     nc.tensor.transpose(out=trp[:, q4, :], in_=xr[:, (4 * a + q4) * P : (4 * a + q4 + 1) * P], identity=ident[:])
                 nc.scalar.copy(out=xg_v[:, 2 * a : 2 * a + 2], in_=trp[:].rearrange("p (jl u) m -> p jl m u", u=2))
-            xg_of[g] = xg
-            xq[g] = xpool.tile([P, 1024], U32, name="xq%d" % g, tag="xq%d" % g, align_bytes=64)
-            xs[g] = xpool.tile([P, 1024], U8, name="xs%d" % g, tag="xs%d" % g, align_bytes=64)
 
         def x_quant(g, n):
             nc.vector.quantize_mx(
@@ -416,78 +398,29 @@ def tile_attentionconv_kernel(tc, x, W_qkv_bytes, W_qkv_scale, b_qkv, out):
         def ok(t):
             return 0 <= t < NT
 
-        if QA == 4:
-            w_scale(0)
-            bias_consts()
-            w_turn(0)
-            w_scale(1)
-            w_quant(0)
-            x_reorder(0)
-            w_turn(1)
-            w_scale(2)
-            w_quant(1)
-            x_turn(0)
-            x_quant(0, 0)
-            x_quant(0, 1)
-            w_turn(2)
-            w_scale(3)
-            w_quant(2)
-            x_reorder(1)
-            x_turn(1)
-            w_turn(3)
-            w_scale(4)
-            x_quant(1, 0)
-            x_quant(1, 1)
-            w_quant(3)
-        elif QA == 3:
-            w_scale(0)
-            bias_consts()
-            w_turn(0)
-            w_scale(1)
-            w_quant(0)
-            x_reorder(0)
-            w_turn(1)
-            w_scale(2)
-            w_quant(1)
-            x_turn(0)
-            x_quant(0, 0)
-            x_quant(0, 1)
-            w_scale(3)
-            x_reorder(1)
-            x_turn(1)
-            if PAX >= 2:
-                w_scale(4)
-            x_quant(1, 0)
-            x_quant(1, 1)
-            w_turn(2)
-            w_quant(2)
-        else:
-            if BIAS_FIRST:
-                bias_consts()
-            w_scale(0)
-            if not BIAS_FIRST:
-                bias_consts()
-            w_turn(0)
-            x_reorder(0)
-            w_scale(1)
-            w_quant(0)
-            x_turn(0)
-            x_reorder(1)
-            w_turn(1)
-            x_quant(0, 0)
-            x_quant(0, 1)
-            x_turn(1)
-            w_scale(2)
-            w_quant(1)
-            x_quant(1, 0)
-            x_quant(1, 1)
+        w_scale(0)
+        bias_consts()
+        x_reorder(0, (0,))
+        w_turn(0)
+        w_scale(1)
+        w_quant(0)
+        x_reorder(0, (1,))
+        w_turn(1)
+        w_scale(2)
+        w_quant(1)
+        x_turn(0)
+        x_quant(0, 0)
+        x_quant(0, 1)
+        x_reorder(1, (0,))
+        w_scale(3)
+        x_reorder(1, (1,))
+        x_turn(1)
+        x_quant(1, 0)
+        x_quant(1, 1)
+        w_turn(2)
+        w_quant(2)
         ring(0)
         mx_kv(0)
-        if PAX >= 3:
-            w_scale(QA + 2)
-        if not DEEP:
-            mx_q(0)
-            q_bias(0)
 
         def last_stores(t, n):
             if TAIL_SPLIT and t == NT - 1:

@@ -17,21 +17,7 @@ FLOPS = 2 * 1024 * 1024 * 3072
 
 P = 128
 NT = 8
-LATE = 4
-LATE_HALVES = (0, 1)
-UPPER_TS = False
-RING_POOL = False
-XR_V = 0
-QA = 3
-NB_WHOLE = False
-QLAST = False
-PAX = 1
-DEEP = True
-UB = 3
-KQB = 4
-TTB = 3
-TAIL_SPLIT = False
-QUANT_WIDE_FROM = 2
+LATE = 6
 
 
 def tile_attentionconv_kernel(tc, x, W_qkv_bytes, W_qkv_scale, b_qkv, out):
@@ -40,7 +26,7 @@ def tile_attentionconv_kernel(tc, x, W_qkv_bytes, W_qkv_scale, b_qkv, out):
         const = ctx.enter_context(tc.tile_pool(name="const", bufs=1))
         xpool = ctx.enter_context(tc.tile_pool(name="xpool", bufs=1))
         wkeep = ctx.enter_context(tc.tile_pool(name="wkeep", bufs=1))
-        wwork = ctx.enter_context(tc.tile_pool(name="wwork", bufs=3))
+        wwork = ctx.enter_context(tc.tile_pool(name="wwork", bufs=2))
         epi = ctx.enter_context(tc.tile_pool(name="epi", bufs=2))
         ps = ctx.enter_context(tc.psum_pool(name="ps", bufs=2))
         ctx.enter_context(tc.manual_schedule())
@@ -52,42 +38,57 @@ def tile_attentionconv_kernel(tc, x, W_qkv_bytes, W_qkv_scale, b_qkv, out):
         brow = const.tile([P, P], BF16, name="brow", tag="brow")
         nc.gpsimd.memset(brow[:], 0.0)
         b_rows = b_qkv.rearrange("(w m) -> w m", m=P)
-        nc.sync.dma_start(out=srow[0:8, :], in_=W_qkv_scale.rearrange("o (m n) -> (o m) n", n=P))
-
+        scale_bc = const.tile([P, 1024], F32, name="scale_bc", tag="scale_bc")
         w_rows = W_qkv_bytes.rearrange("(w m) k -> m w k", m=P)
         wbytes = {}
-
-        def load_w(t):
-            wb = wkeep.tile([P, 3, 1024], U8, name="wbytes%d" % t, tag="wbytes%d" % t)
-            nc.sync.dma_start(out=wb[:], in_=w_rows[:, t : 24 : NT, :])
-            wbytes[t] = wb
-
         xin = {}
 
-        def load_x(ch):
-            xt = xpool.tile([P, 2048], BF16, name="xin%d" % ch, tag="xin%d" % ch)
-            for b in range(4):
-                src = x[b, ch].rearrange("(i r) (jh w) -> jh i r w", r=16, jh=2)
-                for jh in range(2):
-                    nc.sync.dma_start(
-                        out=xt[64 * jh + b : 64 * (jh + 1) : 4, :].rearrange("p (r w) -> p r w", r=16),
-                        in_=src[jh],
-                    )
-            xin[ch] = xt
+        def load_scale_rows():
+            nc.sync.dma_start(out=srow[0:8, :], in_=W_qkv_scale.rearrange("o (m n) -> (o m) n", n=P))
 
-        for kind, idx in [("w", 0), ("x", 0), ("b", 0), ("w", 1), ("x", 1), ("w", 2), ("x", 2), ("x", 3), ("w", 3), ("w", 4), ("w", 5), ("w", 6), ("w", 7)]:
-            if kind == "w":
-                load_w(idx)
-            elif kind == "x":
-                load_x(idx)
-            else:
-                nc.sync.dma_start(out=brow[0:16, :], in_=b_rows[0:16, :])
-                nc.sync.dma_start(out=brow[16:24, :], in_=b_rows[16:24, :])
+        def load_scale_bc():
+            nc.sync.dma_start(out=scale_bc[:, 0:512], in_=W_qkv_scale.rearrange("o k -> (o k)")[0:512].partition_broadcast(P))
+
+        def load_bias():
+            nc.sync.dma_start(out=brow[0:16, :], in_=b_rows[0:16, :])
+            nc.sync.dma_start(out=brow[16:24, :], in_=b_rows[16:24, :])
+
+        def load_w(t):
+            wbytes[t] = wkeep.tile([P, 3, 1024], U8, name="wbytes%d" % t, tag="wbytes%d" % t)
+            nc.sync.dma_start(out=wbytes[t][:], in_=w_rows[:, t : 24 : NT, :])
+
+        def load_w_rows(t, js):
+            if t not in wbytes:
+                wbytes[t] = wkeep.tile([P, 3, 1024], U8, name="wbytes%d" % t, tag="wbytes%d" % t)
+            nc.sync.dma_start(out=wbytes[t][:, js, :], in_=w_rows[:, t : 24 : NT, :][:, js, :])
+
+        def load_x(n, c, queue=nc.sync):
+            xin[(n, c)] = xpool.tile([P, 2048], BF16, name="xin%d%d" % (n, c), tag="xin%d%d" % (n, c))
+            for b in range(4):
+                for g in range(2):
+                    queue.dma_start(
+                        out=xin[(n, c)][64 * g + b : 64 * (g + 1) : 4, :].rearrange("p (r w) -> p r w", r=16),
+                        in_=x[b, 2 * g + c].rearrange("(i r) (jh w) -> jh i r w", r=16, jh=2)[n],
+                    )
 
         ident = const.tile([P, P], F32, name="ident", tag="ident")
         make_identity(nc, ident[:])
         identb = const.tile([P, P], BF16, name="identb", tag="identb")
         make_identity(nc, identb[:])
+        load_scale_rows()
+        load_w_rows(0, slice(0, 1))
+        load_scale_bc()
+        load_w_rows(0, slice(1, 3))
+        load_bias()
+        load_x(0, 0)
+        load_w(1)
+        load_x(0, 1)
+        load_x(1, 1)
+        load_w(2)
+        for t in range(3, NT):
+            load_w(t)
+        load_x(1, 0, nc.gpsimd)
+
         zeros = const.tile([P, P], F32, name="zeros", tag="zeros")
         nc.vector.memset(zeros[:], 0.0)
 
@@ -108,134 +109,127 @@ def tile_attentionconv_kernel(tc, x, W_qkv_bytes, W_qkv_scale, b_qkv, out):
         nc.scalar.activation(out=cf[:], in_=args[:], func=ACT.Exp)
         c0 = cf[:, 0:1]
         c2 = cf[:, 1:2]
-        csum = const.tile([P, 1], F32, name="csum", tag="csum")
-        nc.vector.scalar_tensor_tensor(out=csum[:], in0=c0, scalar=1.0, in1=c2, op0=ALU.add, op1=ALU.add)
 
-        scale_bc = const.tile([P, 1024], F32, name="scale_bc", tag="scale_bc")
         scol = const.tile([P, 8], F32, name="scol", tag="scol")
         sps = ps.tile([P, P], F32, name="sps", tag="ev", bufs=4)
         nc.tensor.transpose(out=sps[:], in_=srow[:], identity=ident[:])
         nc.vector.tensor_copy(out=scol[:], in_=sps[:, 0:8])
-        for h in range(2):
+        for h in range(512 // 512, 2):
             spb = ps.tile([P, 4, P], F32, name="spb", tag="ev", bufs=4)
             for q4 in range(4):
                 m = 4 * h + q4
                 nc.tensor.transpose(out=spb[:, q4, :], in_=scol[:, m : m + 1].to_broadcast([P, P]), identity=ident[:])
-            if h == 0:
-                nc.vector.tensor_copy(out=scale_bc[:, 0:512], in_=spb[:].rearrange("p q n -> p (q n)"))
-            else:
-                nc.scalar.copy(out=scale_bc[:, 512:1024], in_=spb[:].rearrange("p q n -> p (q n)"))
+            (nc.vector.tensor_copy if h == 0 else nc.scalar.copy)(
+                out=scale_bc[:, 512 * h : 512 * (h + 1)], in_=spb[:].rearrange("p q n -> p (q n)")
+            )
 
+        csum = const.tile([P, 1], F32, name="csum", tag="csum")
+        nc.vector.scalar_tensor_tensor(out=csum[:], in0=c0, scalar=1.0, in1=c2, op0=ALU.add, op1=ALU.add)
         b_f = const.tile([P, 24], F32, name="b_f", tag="b_f")
         bkbv = const.tile([P, NT], F32, name="bkbv", tag="bkbv")
         tbord = const.tile([P, NT], F32, name="tbord", tag="tbord")
         ub0 = const.tile([P, NT], F32, name="ub0", tag="ub0")
         ub2 = const.tile([P, NT], F32, name="ub2", tag="ub2")
+        bps_of = {}
 
-        def bias_consts():
-            bps = ps.tile([P, P], BF16, name="bps", tag="ev", bufs=4)
-            nc.tensor.transpose(out=bps[:], in_=brow[:], identity=identb[:])
-            nc.vector.tensor_copy(out=b_f[:], in_=bps[:, 0:24])
-            eng = nc.vector
-            eng.tensor_tensor(out=bkbv[:], in0=b_f[:, 8:16], in1=b_f[:, 16:24], op=ALU.mult)
-            eng.tensor_scalar(out=tbord[:], in0=bkbv[:], scalar1=csum[:], scalar2=None, op0=ALU.mult)
+        def bias_turn():
+            bps_of[0] = ps.tile([P, P], BF16, name="bps", tag="ev", bufs=4)
+            nc.tensor.transpose(out=bps_of[0][:], in_=brow[:], identity=identb[:])
+
+        def bias1():
+            nc.vector.tensor_copy(out=b_f[:], in_=bps_of[0][:, 0:24])
+
+        def bias2():
+            nc.vector.tensor_tensor(out=bkbv[:], in0=b_f[:, 8:16], in1=b_f[:, 16:24], op=ALU.mult)
+
+        def bias3():
+            nc.vector.tensor_scalar(out=tbord[:], in0=bkbv[:], scalar1=csum[:], scalar2=None, op0=ALU.mult)
+
+        def bias4():
             for rh in range(2):
-                eng.tensor_scalar(out=ub0[:, rh:NT:2], in0=tbord[:, rh:NT:2], scalar1=cf[:, 2 + rh : 3 + rh], scalar2=None, op0=ALU.mult)
-                eng.tensor_scalar(out=ub2[:, rh:NT:2], in0=tbord[:, rh:NT:2], scalar1=cf[:, 4 + rh : 5 + rh], scalar2=None, op0=ALU.mult)
+                nc.vector.tensor_scalar(out=ub0[:, rh:NT:2], in0=tbord[:, rh:NT:2], scalar1=cf[:, 2 + rh : 3 + rh], scalar2=None, op0=ALU.mult)
+                nc.vector.tensor_scalar(out=ub2[:, rh:NT:2], in0=tbord[:, rh:NT:2], scalar1=cf[:, 4 + rh : 5 + rh], scalar2=None, op0=ALU.mult)
 
         wsc_of = {}
         wg_of = {}
         wq = {}
         ws = {}
 
-        def w_scale(t):
-            wsc = wwork.tile([P, 3, 1024], BF16, name="wsc", tag="wsc", bufs=max(2, PAX))
-            for j in range(3):
-                for ks in [slice(0, 512), slice(512, 1024)] if t == 0 and j == 0 else [slice(0, 1024)]:
-                    nc.vector.tensor_tensor(out=wsc[:, j, ks], in0=wbytes[t][:, j, ks].bitcast(FP8), in1=scale_bc[:, ks], op=ALU.mult)
-                wsc_of[(t, j)] = wsc[:, j, :]
+        def w_scale(t, js=(0, 1, 2), hs=(0, 1)):
+            if t not in wsc_of:
+                wsc_of[t] = wwork.tile([P, 3, 1024], BF16, name="wsc", tag="wsc", bufs=2)
+            ks = slice(512 * hs[0], 512 * (hs[-1] + 1))
+            for j in js:
+                nc.vector.tensor_tensor(out=wsc_of[t][:, j, ks], in0=wbytes[t][:, j, ks].bitcast(FP8), in1=scale_bc[:, ks], op=ALU.mult)
 
         def w_turn(t, js=(0, 1, 2)):
             if t not in wg_of:
-                wg_of[t] = wwork.tile([P, 3072], BF16, name="wg3", tag="wg", align_bytes=64, bufs=2)
-            wg3 = wg_of[t]
+                wg_of[t] = wwork.tile([P, 3072], BF16, name="wg", tag="wg", align_bytes=64, bufs=2)
             for j in js:
-                words = wsc_of[(t, j)].bitcast(F32)
+                words = wsc_of[t][:, j, :].bitcast(F32)
                 trp = ps.tile([P, 4, P], F32, name="trp", tag="ev", bufs=4)
                 for g in range(2):
                     for u in range(2):
                         nc.tensor.transpose(out=trp[:, 2 * g + u, :], in_=words[:, 256 * g + u : 256 * (g + 1) : 2], identity=ident[:])
-                wg = wg3[:, 1024 * j : 1024 * (j + 1)]
                 nc.scalar.copy(
-                    out=wg.bitcast(F32).rearrange("p (g m u) -> p g m u", g=2, u=2),
+                    out=wg_of[t][:, 1024 * j : 1024 * (j + 1)].bitcast(F32).rearrange("p (g m u) -> p g m u", g=2, u=2),
                     in_=trp[:].rearrange("p (g u) m -> p g m u", g=2),
                 )
-        def w_quant(t):
-            wq_t = wkeep.tile([P, 768], U32, name="wq%d" % t, tag="wq%d" % t, align_bytes=64)
-            ws_t = wkeep.tile([P, 768], U8, name="ws%d" % t, tag="ws%d" % t, align_bytes=64)
-            for c0w, c1w in ([(0, 512), (512, 768)] if t >= QUANT_WIDE_FROM else [(0, 256), (256, 512), (512, 768)]):
-                nc.vector.quantize_mx(
-                    out=wq_t[:, c0w:c1w].bitcast(FP8X4),
-                    scales=ws_t[:, c0w:c1w],
-                    in_=wg_of[t][:, 4 * c0w : 4 * c1w],
-                )
-            wq[t] = wq_t
-            ws[t] = ws_t
 
-        xr_of = {}
-        xg_of = {}
+        def w_quant(t, part=(0, 1)):
+            if t not in wq:
+                wq[t] = wkeep.tile([P, 768], U32, name="wq%d" % t, tag="wq%d" % t, align_bytes=64)
+                ws[t] = wkeep.tile([P, 768], U8, name="ws%d" % t, tag="ws%d" % t, align_bytes=64)
+            for i in part:
+                cols = slice(0, 512) if i == 0 else slice(512, 768)
+                nc.vector.quantize_mx(
+                    out=wq[t][:, cols].bitcast(FP8X4), scales=ws[t][:, cols], in_=wg_of[t][:, 4 * cols.start : 4 * cols.stop]
+                )
+
+        xr = {}
+        xg = {}
         xq = {}
         xs = {}
+        for n in range(2):
+            xr[n] = xpool.tile([P, 2048], F32, name="xr%d" % n, tag="xr%d" % n)
+            xg[n] = xpool.tile([P, 2, 2048], BF16, name="xg%d" % n, tag="xg%d" % n, align_bytes=64)
+            for g in range(2):
+                xq[(g, n)] = xpool.tile([P, 512], U32, name="xq%d%d" % (g, n), tag="xq%d%d" % (g, n), align_bytes=64)
+                xs[(g, n)] = xpool.tile([P, 512], U8, name="xs%d%d" % (g, n), tag="xs%d%d" % (g, n), align_bytes=64)
 
-        def x_reorder(g, cs=(0, 1)):
-            if g not in xr_of:
-                xr_of[g] = xpool.tile([P, 2048], F32, name="xr%d" % g, tag="xr%d" % g)
-            xr = xr_of[g]
-            xr_v = xr[:].rearrange("p (jl u c2 r s4) -> p u c2 jl r s4", jl=8, u=2, c2=2, r=16)
-            for c2i in cs:
-                xw = xin[2 * g + c2i][:].bitcast(F32).rearrange("p (r jl s4 u) -> p u jl r s4", r=16, jl=8, s4=4)
-                for u in range(2):
-                    if 2 * c2i + u < XR_V:
-                        nc.vector.tensor_copy(out=xr_v[:, u, c2i], in_=xw[:, u])
-                    else:
-                        nc.scalar.copy(out=xr_v[:, u, c2i], in_=xw[:, u])
-        def x_turn(g, part=(0, 1, 2, 3)):
-            xr = xr_of[g]
-            if g not in xg_of:
-                xg_of[g] = xpool.tile([P, 4096], BF16, name="xg%d" % g, tag="xg%d" % g, align_bytes=64)
-                xq[g] = xpool.tile([P, 1024], U32, name="xq%d" % g, tag="xq%d" % g, align_bytes=64)
-                xs[g] = xpool.tile([P, 1024], U8, name="xs%d" % g, tag="xs%d" % g, align_bytes=64)
-            xg = xg_of[g]
-            xg_v = xg[:].bitcast(F32).rearrange("p (jl m u) -> p jl m u", jl=8, u=2)
-            for a in part:
+        def x_reorder(n, c, engines="ss"):
+            xr_v = xr[n][:].rearrange("p (jl u c r s4) -> p u c jl r s4", jl=8, u=2, c=2, r=16)
+            xw = xin[(n, c)][:].bitcast(F32).rearrange("p (r jl s4 u) -> p u jl r s4", r=16, jl=8, s4=4)
+            for u in range(2):
+                if engines[u] == "v":
+                    nc.vector.tensor_copy(out=xr_v[:, u, c], in_=xw[:, u])
+                elif engines[u] == "s":
+                    nc.scalar.copy(out=xr_v[:, u, c], in_=xw[:, u])
+
+        def x_turn(n, parts=(0, 1, 2, 3)):
+            xg_v = xg[n][:].bitcast(F32).rearrange("p g (a jl m u) -> p a g jl m u", a=4, jl=2, u=2)
+            for a in parts:
                 trp = ps.tile([P, 4, P], F32, name="trp", tag="ev", bufs=4)
                 for q4 in range(4):
-                    nc.tensor.transpose(out=trp[:, q4, :], in_=xr[:, (4 * a + q4) * P : (4 * a + q4 + 1) * P], identity=ident[:])
-                nc.scalar.copy(out=xg_v[:, 2 * a : 2 * a + 2], in_=trp[:].rearrange("p (jl u) m -> p jl m u", u=2))
+                    nc.tensor.transpose(out=trp[:, q4, :], in_=xr[n][:, P * (4 * a + q4) : P * (4 * a + q4 + 1)], identity=ident[:])
+                nc.scalar.copy(out=xg_v[:, a], in_=trp[:].rearrange("p (jl u) (g m) -> p g jl m u", u=2, g=2))
 
-        def x_quant(g, n):
-            nc.vector.quantize_mx(
-                out=xq[g][:, 512 * n : 512 * (n + 1)].bitcast(FP8X4),
-                scales=xs[g][:, 512 * n : 512 * (n + 1)],
-                in_=xg_of[g][:, 2048 * n : 2048 * (n + 1)],
-            )
+        def x_quant(n, g):
+            nc.vector.quantize_mx(out=xq[(g, n)][:].bitcast(FP8X4), scales=xs[(g, n)][:], in_=xg[n][:, g, :])
 
         def project(t, j, n, tag):
             acc = ps.tile([P, 512], F32, name="acc_" + tag, tag=tag, bufs=(4 if tag == "ev" else 2))
             for g in range(2):
                 cols = slice(256 * j + P * g, 256 * j + P * (g + 1))
                 nc.tensor.matmul_mx(
-                    out=acc[:],
-                    lhsT=wq[t][:, cols].bitcast(FP8X4),
-                    lhsT_scale=ws[t][:, cols],
-                    rhs=xq[g][:, 512 * n : 512 * (n + 1)].bitcast(FP8X4),
-                    rhs_scale=xs[g][:, 512 * n : 512 * (n + 1)],
-                    start=(g == 0),
-                    stop=(g == 1),
+                    out=acc[:], lhsT=wq[t][:, cols].bitcast(FP8X4), lhsT_scale=ws[t][:, cols],
+                    rhs=xq[(g, n)][:].bitcast(FP8X4), rhs_scale=xs[(g, n)][:], start=(g == 0), stop=(g == 1),
                 )
             return acc
 
         kvp_of = {}
+        tmp_of = {}
+        tt_of = {}
         u0_of = {}
         u2_of = {}
         kp_of = {}
@@ -243,239 +237,201 @@ def tile_attentionconv_kernel(tc, x, W_qkv_bytes, W_qkv_scale, b_qkv, out):
         qacc_of = {}
         qp_of = {}
         qts_of = {}
-        tmp_of = {}
-        tt_of = {}
         stp_of = {}
         ot_of = {}
-        zb = zeros[:, 0:64].rearrange("p (a c) -> p a c", c=4)
-
-        def v_halves(t):
-            return LATE_HALVES if t >= LATE and not UPPER_TS else ()
 
         def fill(dst, src, col):
-            if RING_POOL:
-                nc.gpsimd.tensor_scalar(out=dst, in0=src, scalar1=1.0, scalar2=col, op0=ALU.mult, op1=ALU.add)
-            else:
-                nc.scalar.activation(out=dst, in_=src, func=ACT.Identity, bias=col, scale=1.0)
+            nc.scalar.activation(out=dst, in_=src, func=ACT.Identity, bias=col, scale=1.0)
 
         def ring(t):
-            kvp = epi.tile([P, 1152], F32, name="kvp", tag="kvp")
-            fill(kvp[:].rearrange("p (k c) -> p k c", c=64)[:, 0:18:17, :], zeros[:].rearrange("p (a c) -> p a c", c=64), bkbv[:, t : t + 1])
+            kvp = epi.tile([P, 18, 64], F32, name="kvp", tag="kvp", bufs=2)
+            fill(kvp[:, 0:18:17, :], zeros[:].rearrange("p (a c) -> p a c", c=64), bkbv[:, t : t + 1])
             kvp_of[t] = kvp
-            u2 = epi.tile([P, 16, 64], F32, name="u2", tag="u2", bufs=UB)
-            fill(u2[:, :, 60:64], zb, ub2[:, t : t + 1])
-            u2_of[t] = u2
-            u0 = epi.tile([P, 16, 64], F32, name="u0", tag="u0", bufs=UB)
-            u0_of[t] = u0
-            if len(v_halves(t)) == 0:
-                fill(u0[:, :, 0:4], zb, ub0[:, t : t + 1])
-            else:
-                for n in range(2):
-                    if n not in v_halves(t):
-                        fill(u0[:, 8 * n : 8 * (n + 1), 0:4], zeros[:, 0:32].rearrange("p (a c) -> p a c", c=4), ub0[:, t : t + 1])
+            zb = zeros[:, 0:64].rearrange("p (a c) -> p a c", c=4)
+            u2_of[t] = epi.tile([P, 16, 64], F32, name="u2", tag="u2", bufs=3)
+            fill(u2_of[t][:, :, 60:64], zb, ub2[:, t : t + 1])
+            u0_of[t] = epi.tile([P, 16, 64], F32, name="u0", tag="u0", bufs=3)
+            if t < LATE:
+                fill(u0_of[t][:, :, 0:4], zb, ub0[:, t : t + 1])
 
-        def mx_kv(t):
-            for n in range(2):
-                kacc = project(t, 1, n, "ev")
-                vacc_of[(t, n)] = project(t, 2, n, "v")
-                kp = epi.tile([P, 512], F32, name="kp", tag="kp", bufs=KQB)
-                nc.scalar.activation(out=kp[:], in_=kacc[:], func=ACT.Identity, bias=b_f[:, 8 + t : 9 + t], scale=1.0)
-                kp_of[(t, n)] = kp
+        def mx_kv(t, n):
+            kacc = project(t, 1, n, "ev")
+            vacc_of[(t, n)] = project(t, 2, n, "v")
+            kp = epi.tile([P, 512], F32, name="kp", tag="kp", bufs=4)
+            nc.scalar.activation(out=kp[:], in_=kacc[:], func=ACT.Identity, bias=b_f[:, 8 + t : 9 + t], scale=1.0)
+            kp_of[(t, n)] = kp
 
-        def mx_q(t):
-            for n in range(2):
-                qacc_of[(t, n)] = project(t, 0, n, "ev")
+        def mx_q(t, n):
+            qacc_of[(t, n)] = project(t, 0, n, "ev")
 
-        def q_bias(t):
-            for n in range(2):
-                qp = epi.tile([P, 512], F32, name="qp", tag="qp", bufs=KQB)
-                nc.scalar.activation(out=qp[:], in_=qacc_of[(t, n)][:], func=ACT.Identity, bias=b_f[:, t : t + 1], scale=1.0)
-                qp_of[(t, n)] = qp
+        def q_bias(t, n):
+            if t not in qp_of:
+                qp_of[t] = epi.tile([P, 8, 2, 64], F32, name="qp", tag="qp", bufs=2)
+            nc.scalar.activation(
+                out=qp_of[t][:, :, n, :], in_=qacc_of[(t, n)][:].rearrange("p (jl m) -> p jl m", m=64), func=ACT.Identity, bias=b_f[:, t : t + 1], scale=1.0
+            )
 
-        def kv_mul(t):
-            for n in range(2):
-                nc.vector.scalar_tensor_tensor(
-                    out=kvp_of[t][:, 64 + 512 * n : 64 + 512 * (n + 1)], in0=vacc_of[(t, n)][:], scalar=b_f[:, 16 + t : 17 + t],
-                    in1=kp_of[(t, n)][:], op0=ALU.add, op1=ALU.mult,
-                )
+        def kv_mul(t, n):
+            nc.vector.scalar_tensor_tensor(
+                out=kvp_of[t][:, 1 + n : 17 : 2, :], in0=vacc_of[(t, n)][:].rearrange("p (jl m) -> p jl m", m=64), scalar=b_f[:, 16 + t : 17 + t],
+                in1=kp_of[(t, n)][:].rearrange("p (jl m) -> p jl m", m=64), op0=ALU.add, op1=ALU.mult,
+            )
 
-        def q_turn(t):
-            for n in range(2):
-                qtp = ps.tile([P, 4, P], F32, name="qtp", tag="ev", bufs=4)
-                for q4 in range(4):
-                    nc.tensor.transpose(out=qtp[:, q4, :], in_=qp_of[(t, n)][:, P * q4 : P * (q4 + 1)], identity=ident[:])
-                qts = epi.tile([P, 512], F32, name="qts", tag="qts", bufs=4)
-                nc.scalar.copy(out=qts[:], in_=qtp[:].rearrange("p jl e -> p (jl e)"))
-                qts_of[(t, n)] = qts
+        def q_turn(t, h):
+            qp = qp_of[t][:].rearrange("p jl n m -> p (jl n m)")
+            qtp = ps.tile([P, 4, P], F32, name="qtp", tag="ev", bufs=4)
+            for q4 in range(4):
+                nc.tensor.transpose(out=qtp[:, q4, :], in_=qp[:, P * (4 * h + q4) : P * (4 * h + q4 + 1)], identity=ident[:])
+            qts = epi.tile([P, 512], F32, name="qts", tag="qts", bufs=4)
+            nc.scalar.copy(out=qts[:], in_=qtp[:].rearrange("p jl e -> p (jl e)"))
+            qts_of[(t, h)] = qts
 
         def h1(t):
             kvp = kvp_of[t]
-            kvb = kvp[:].rearrange("p (k c) -> p k c", c=64)
+            kvf = kvp[:].rearrange("p k m -> p (k m)")
             tmp = epi.tile([P, 1024], F32, name="tmp", tag="tmp", bufs=1)
-            nc.vector.scalar_tensor_tensor(out=tmp[:, 128:1024], in0=kvp[:, 64:960], scalar=c0, in1=kvp[:, 192:1088], op0=ALU.mult, op1=ALU.add)
+            nc.vector.scalar_tensor_tensor(out=tmp[:, 128:1024], in0=kvf[:, 64:960], scalar=c0, in1=kvf[:, 192:1088], op0=ALU.mult, op1=ALU.add)
             nc.vector.scalar_tensor_tensor(
-                out=tmp[:, 0:128].rearrange("p (k c) -> p k c", c=64), in0=kvb[:, 0:16:15, :], scalar=c0, in1=kvb[:, 1:3, :],
+                out=tmp[:, 0:128].rearrange("p (k c) -> p k c", c=64), in0=kvp[:, 0:16:15, :], scalar=c0, in1=kvp[:, 1:3, :],
                 op0=ALU.mult, op1=ALU.add,
             )
             tmp_of[t] = tmp
 
         def h2(t):
             kvp = kvp_of[t]
-            kvb = kvp[:].rearrange("p (k c) -> p k c", c=64)
+            kvf = kvp[:].rearrange("p k m -> p (k m)")
             tmp = tmp_of[t]
-            tt = epi.tile([P, 1024], F32, name="tt", tag="tt", bufs=TTB)
-            nc.vector.scalar_tensor_tensor(out=tt[:, 0:896], in0=kvp[:, 192:1088], scalar=c2, in1=tmp[:, 0:896], op0=ALU.mult, op1=ALU.add)
+            tt = epi.tile([P, 1024], F32, name="tt", tag="tt", bufs=3)
+            nc.vector.scalar_tensor_tensor(out=tt[:, 0:896], in0=kvf[:, 192:1088], scalar=c2, in1=tmp[:, 0:896], op0=ALU.mult, op1=ALU.add)
             nc.vector.scalar_tensor_tensor(
-                out=tt[:, 896:1024].rearrange("p (k c) -> p k c", c=64), in0=kvb[:, 2:18:15, :], scalar=c2,
+                out=tt[:, 896:1024].rearrange("p (k c) -> p k c", c=64), in0=kvp[:, 2:18:15, :], scalar=c2,
                 in1=tmp[:, 896:1024].rearrange("p (k c) -> p k c", c=64), op0=ALU.mult, op1=ALU.add,
             )
             tt_of[t] = tt
 
-        def upper_tap(t):
+        def upper_tap(t, ks=slice(0, 16)):
             rh = t % 2
             tv = tt_of[t][:].rearrange("p (k c) -> p k c", c=64)
-            if UPPER_TS:
-                nc.vector.tensor_scalar(out=u0_of[t][:, :, 4:64], in0=tv[:, :, 0:60], scalar1=cf[:, 2 + rh : 3 + rh], scalar2=None, op0=ALU.mult)
-                return
-            yy = u0_of[t]
-            for ks in ([slice(0, 16)] if len(v_halves(t)) == 2 else [slice(8 * n, 8 * (n + 1)) for n in v_halves(t)]):
-                nc.vector.scalar_tensor_tensor(
-                    out=yy[:, ks, 4:64], in0=tv[:, ks, 0:60], scalar=cf[:, 2 + rh : 3 + rh], in1=tv[:, ks, 4:64], op0=ALU.mult, op1=ALU.add,
-                )
-                nc.vector.tensor_scalar(out=yy[:, ks, 0:4], in0=tv[:, ks, 0:4], scalar1=ub0[:, t : t + 1], scalar2=None, op0=ALU.add)
+            nc.vector.scalar_tensor_tensor(
+                out=u0_of[t][:, ks, 4:64], in0=tv[:, ks, 0:60], scalar=cf[:, 2 + rh : 3 + rh], in1=tv[:, ks, 4:64], op0=ALU.mult, op1=ALU.add,
+            )
+            nc.vector.tensor_scalar(out=u0_of[t][:, ks, 0:4], in0=tv[:, ks, 0:4], scalar1=ub0[:, t : t + 1], scalar2=None, op0=ALU.add)
 
-        def neighbours(t):
+        def neighbours(t, h):
             rh = t % 2
             tv = tt_of[t][:].rearrange("p (k c) -> p k c", c=64)
-            halves = [slice(8 * n, 8 * (n + 1)) for n in range(2)]
-            up = [halves[n] for n in range(2) if n not in v_halves(t) and not (UPPER_TS and t >= LATE)]
-            down = halves
-            if NB_WHOLE:
-                down = [slice(0, 16)]
-                if len(up) == 2:
-                    up = [slice(0, 16)]
-            for ks in down:
-                for ku in up:
-                    if ku.start == ks.start or (NB_WHOLE and ks.start == 0):
-                        nc.scalar.activation(out=u0_of[t][:, ku, 4:64], in_=tv[:, ku, 0:60], func=ACT.Copy, scale=cf[:, 2 + rh : 3 + rh])
-                nc.scalar.activation(out=u2_of[t][:, ks, 0:60], in_=tv[:, ks, 4:64], func=ACT.Copy, scale=cf[:, 4 + rh : 5 + rh])
+            ks = slice(8 * h, 8 * (h + 1))
+            if t < LATE:
+                nc.scalar.activation(out=u0_of[t][:, ks, 4:64], in_=tv[:, ks, 0:60], func=ACT.Copy, scale=cf[:, 2 + rh : 3 + rh])
+            nc.scalar.activation(out=u2_of[t][:, ks, 0:60], in_=tv[:, ks, 4:64], func=ACT.Copy, scale=cf[:, 4 + rh : 5 + rh])
 
-        def vertical(t):
-            u0 = u0_of[t][:].rearrange("p k c -> p (k c)")
-            u2 = u2_of[t][:].rearrange("p k c -> p (k c)")
-            for n in range(2):
-                stp = ps.tile([P, 4, P], F32, name="stp", tag="sT", bufs=2)
-                for q4 in range(4):
-                    cols = slice(P * (4 * n + q4), P * (4 * n + q4 + 1))
-                    three = n not in v_halves(t)
-                    if three:
-                        nc.tensor.matmul(out=stp[:, q4, :], lhsT=tt_of[t][:, cols], rhs=ident[:], start=True, stop=False, is_transpose=True)
-                    nc.tensor.matmul(out=stp[:, q4, :], lhsT=u0[:, cols], rhs=ident[:], start=(not three), stop=False, is_transpose=True)
-                    nc.tensor.matmul(out=stp[:, q4, :], lhsT=u2[:, cols], rhs=ident[:], start=False, stop=True, is_transpose=True)
-                stp_of[(t, n)] = stp
+        def vertical(t, h):
+            terms = ([tt_of[t][:]] if t < LATE else []) + [u_of[t][:].rearrange("p k c -> p (k c)") for u_of in (u0_of, u2_of)]
+            stp = ps.tile([P, 4, P], F32, name="stp", tag="sT", bufs=2)
+            for q4 in range(4):
+                for i, term in enumerate(terms):
+                    nc.tensor.matmul(
+                        out=stp[:, q4, :], lhsT=term[:, P * (4 * h + q4) : P * (4 * h + q4 + 1)], rhs=ident[:],
+                        start=(i == 0), stop=(i == len(terms) - 1), is_transpose=True,
+                    )
+            stp_of[(t, h)] = stp
 
-        def fin(t, n):
-            if n == 0:
+        def fin(t, h):
+            if h == 0:
                 ot_of[t] = epi.tile([P, 1024], F32, name="ot", tag="ot", bufs=3)
-            ot_v = ot_of[t][:].rearrange("p (r jl s) -> p jl r s", r=8, jl=8)
             nc.vector.tensor_tensor(
-                out=ot_v[:, 4 * n : 4 * (n + 1)],
-                in0=stp_of[(t, n)][:].rearrange("p jl (r s) -> p jl r s", s=16),
-                in1=qts_of[(t, n)][:].rearrange("p (jl r s) -> p jl r s", jl=4, s=16),
+                out=ot_of[t][:].rearrange("p (r jl s) -> p jl r s", r=8, jl=8)[:, 4 * h : 4 * (h + 1)],
+                in0=stp_of[(t, h)][:].rearrange("p jl (r s) -> p jl r s", s=16),
+                in1=qts_of[(t, h)][:].rearrange("p (jl r s) -> p jl r s", jl=4, s=16),
                 op=ALU.mult,
             )
 
-        def stores(t, w0=0, w1=128):
+        def stores(t):
             ch, rh = divmod(t, 2)
             for b in range(4):
                 dst = out[b, ch].rearrange("(i r) (jh w) -> jh i r w", r=16, jh=2)
                 for jh in range(2):
                     nc.sync.dma_start(
-                        out=dst[jh, :, 8 * rh : 8 * (rh + 1), w0:w1],
-                        in_=ot_of[t][64 * jh + b : 64 * (jh + 1) : 4, :].rearrange("p (r w) -> p r w", r=8)[:, :, w0:w1],
+                        out=dst[jh, :, 8 * rh : 8 * (rh + 1), :],
+                        in_=ot_of[t][64 * jh + b : 64 * (jh + 1) : 4, :].rearrange("p (r w) -> p r w", r=8),
                     )
 
         def ok(t):
             return 0 <= t < NT
 
-        w_scale(0)
-        bias_consts()
-        x_reorder(0, (0,))
+        w_scale(0, hs=(0,))
+        w_scale(0, hs=(1,))
         w_turn(0)
-        w_scale(1)
-        w_quant(0)
-        x_reorder(0, (1,))
+        bias_turn()
+        x_reorder(0, 0, "vv")
+        bias1()
+        w_scale(1, (0,))
+        bias2()
+        w_scale(1, (1,))
+        bias3()
+        w_scale(1, (2,))
+        bias4()
         w_turn(1)
-        w_scale(2)
-        w_quant(1)
+        x_reorder(0, 1, "vv")
         x_turn(0)
+        x_reorder(1, 0, "vv")
+        w_quant(0)
+        x_reorder(1, 1, "vv")
+        x_turn(1)
+        w_scale(2, (0,))
         x_quant(0, 0)
         x_quant(0, 1)
-        x_reorder(1, (0,))
-        w_scale(3)
-        x_reorder(1, (1,))
-        x_turn(1)
+        w_quant(1)
+        ring(0)
+        mx_kv(0, 0)
+        w_scale(2, (1,))
         x_quant(1, 0)
         x_quant(1, 1)
-        w_turn(2)
-        w_quant(2)
-        ring(0)
-        mx_kv(0)
+        kv_mul(0, 0)
+        mx_kv(0, 1)
+        w_scale(2, (2,))
 
-        def last_stores(t, n):
-            if TAIL_SPLIT and t == NT - 1:
-                stores(t, 64 * n, 64 * (n + 1))
-            elif n == 1:
-                stores(t)
-
-        FD = 2 if DEEP else 1
-        for it in range(0, NT + 1 + (1 if DEEP else 0)):
-            if ok(it + QA):
-                w_turn(it + QA)
+        for it in range(0, NT + 2):
+            if ok(it + 2):
+                w_turn(it + 2)
             if ok(it):
-                kv_mul(it)
-            if ok(it - FD):
-                fin(it - FD, 0)
-                last_stores(it - FD, 0)
-            if ok(it - FD + 1) and not (QLAST and it - FD + 1 == NT - 1):
-                q_turn(it - FD + 1)
+                if it > 0:
+                    kv_mul(it, 0)
+                kv_mul(it, 1)
+            if ok(it - 2):
+                fin(it - 2, 0)
+            if ok(it - 1):
+                q_turn(it - 1, 0)
+                q_turn(it - 1, 1)
+            if ok(it + 3) and it < 2:
+                w_scale(it + 3, (0,))
             if ok(it):
                 h1(it)
-            if ok(it - FD):
-                fin(it - FD, 1)
-                last_stores(it - FD, 1)
+            if ok(it - 2):
+                fin(it - 2, 1)
+                stores(it - 2)
+            if ok(it + 3) and it < 2:
+                w_scale(it + 3, (1,))
             if ok(it):
                 h2(it)
-                if it >= LATE:
-                    upper_tap(it)
             if ok(it + 1):
-                mx_kv(it + 1)
-            if ok(it - FD + 2) and not (QLAST and it - FD + 2 == NT - 1):
-                mx_q(it - FD + 2)
-            if QLAST and it == NT - 2:
-                mx_q(NT - 1)
-            if DEEP:
-                if ok(it) and not (QLAST and it == NT - 1):
-                    q_bias(it)
-                if QLAST and it == NT - 2:
-                    q_bias(NT - 1)
-                if QLAST and it == NT - 1:
-                    q_turn(NT - 1)
-                if ok(it - 1):
-                    vertical(it - 1)
-                if ok(it):
-                    neighbours(it)
-                if ok(it + 1):
-                    ring(it + 1)
-            else:
-                if ok(it):
-                    neighbours(it)
-                if ok(it + 1):
-                    q_bias(it + 1)
-                    ring(it + 1)
-                if ok(it):
-                    vertical(it)
-            if ok(it + QA + PAX):
-                w_scale(it + QA + PAX)
-            if ok(it + QA):
-                w_quant(it + QA)
+                ring(it + 1)
+                mx_kv(it + 1, 0)
+                mx_kv(it + 1, 1)
+            if ok(it):
+                mx_q(it, 0)
+                mx_q(it, 1)
+                q_bias(it, 0)
+                q_bias(it, 1)
+            if ok(it - 1):
+                vertical(it - 1, 0)
+                vertical(it - 1, 1)
+            if ok(it):
+                neighbours(it, 0)
+                neighbours(it, 1)
+            if ok(it + 3):
+                w_scale(it + 3, (2,) if it < 2 else (0, 1, 2))
+            if ok(it + 2):
+                w_quant(it + 2)
+            if ok(it) and it >= LATE:
+                upper_tap(it)

@@ -71,24 +71,25 @@ def tile_attentionconv_kernel(tc, x, W_qkv_bytes, W_qkv_scale, b_qkv, out):
                         in_=x[b, 2 * g + c].rearrange("(i r) (jh w) -> jh i r w", r=16, jh=2)[n],
                     )
 
-        ident = const.tile([P, P], F32, name="ident", tag="ident")
-        make_identity(nc, ident[:])
-        identb = const.tile([P, P], BF16, name="identb", tag="identb")
-        make_identity(nc, identb[:])
         load_scale_rows()
         load_w_rows(0, slice(0, 1))
         load_scale_bc()
         load_w_rows(0, slice(1, 3))
-        load_bias()
-        load_x(0, 0)
         load_w(1)
+        load_x(0, 0)
+        load_bias()
         load_x(0, 1)
-        load_x(1, 1)
         load_w(2)
-        for t in range(3, NT):
+        load_x(1, 0)
+        load_x(1, 1)
+        load_w(3)
+        for t in range(4, NT):
             load_w(t)
-        load_x(1, 0, nc.gpsimd)
 
+        ident = const.tile([P, P], F32, name="ident", tag="ident")
+        make_identity(nc, ident[:])
+        identb = const.tile([P, P], BF16, name="identb", tag="identb")
+        make_identity(nc, identb[:])
         zeros = const.tile([P, P], F32, name="zeros", tag="zeros")
         nc.vector.memset(zeros[:], 0.0)
 
@@ -157,7 +158,7 @@ def tile_attentionconv_kernel(tc, x, W_qkv_bytes, W_qkv_scale, b_qkv, out):
 
         def w_scale(t, js=(0, 1, 2), hs=(0, 1)):
             if t not in wsc_of:
-                wsc_of[t] = wwork.tile([P, 3, 1024], BF16, name="wsc", tag="wsc", bufs=2)
+                wsc_of[t] = wwork.tile([P, 3, 1024], BF16, name="wsc", tag="wsc", bufs=3)
             ks = slice(512 * hs[0], 512 * (hs[-1] + 1))
             for j in js:
                 nc.vector.tensor_tensor(out=wsc_of[t][:, j, ks], in0=wbytes[t][:, j, ks].bitcast(FP8), in1=scale_bc[:, ks], op=ALU.mult)
@@ -244,7 +245,7 @@ def tile_attentionconv_kernel(tc, x, W_qkv_bytes, W_qkv_scale, b_qkv, out):
             nc.scalar.activation(out=dst, in_=src, func=ACT.Identity, bias=col, scale=1.0)
 
         def ring(t):
-            kvp = epi.tile([P, 18, 64], F32, name="kvp", tag="kvp", bufs=2)
+            kvp = epi.tile([P, 18, 64], F32, name="kvp", tag="kvp", bufs=3)
             fill(kvp[:, 0:18:17, :], zeros[:].rearrange("p (a c) -> p a c", c=64), bkbv[:, t : t + 1])
             kvp_of[t] = kvp
             zb = zeros[:, 0:64].rearrange("p (a c) -> p a c", c=4)
@@ -362,76 +363,91 @@ def tile_attentionconv_kernel(tc, x, W_qkv_bytes, W_qkv_scale, b_qkv, out):
         w_scale(0, hs=(0,))
         w_scale(0, hs=(1,))
         w_turn(0)
-        bias_turn()
-        x_reorder(0, 0, "vv")
-        bias1()
+        x_reorder(0, 0, "ss")
         w_scale(1, (0,))
-        bias2()
         w_scale(1, (1,))
-        bias3()
         w_scale(1, (2,))
-        bias4()
-        w_turn(1)
+        w_turn(1, (0, 1))
         x_reorder(0, 1, "vv")
         x_turn(0)
-        x_reorder(1, 0, "vv")
+        bias_turn()
+        w_turn(1, (2,))
         w_quant(0)
-        x_reorder(1, 1, "vv")
-        x_turn(1)
         w_scale(2, (0,))
+        bias1()
+        w_scale(2, (1,))
+        bias2()
         x_quant(0, 0)
+        bias3()
         x_quant(0, 1)
-        w_quant(1)
+        bias4()
         ring(0)
         mx_kv(0, 0)
-        w_scale(2, (1,))
+        x_reorder(1, 0, "vv")
+        x_reorder(1, 1, "vv")
+        x_turn(1)
+        w_quant(1)
+        w_scale(2, (2,))
+        w_turn(2)
+        w_scale(3, (0,))
+        mx_q(0, 0)
+        q_bias(0, 0)
+        kv_mul(0, 0)
         x_quant(1, 0)
         x_quant(1, 1)
-        kv_mul(0, 0)
         mx_kv(0, 1)
-        w_scale(2, (2,))
+        mx_q(0, 1)
+        q_bias(0, 1)
+        w_scale(3, (1,))
+        w_scale(3, (2,))
+        kv_mul(0, 1)
+        mx_kv(1, 0)
+        mx_kv(1, 1)
+        h1(0)
 
         for it in range(0, NT + 2):
-            if ok(it + 2):
-                w_turn(it + 2)
-            if ok(it):
-                if it > 0:
-                    kv_mul(it, 0)
-                kv_mul(it, 1)
-            if ok(it - 2):
-                fin(it - 2, 0)
+            if ok(it + 1):
+                ring(it + 1)
             if ok(it - 1):
                 q_turn(it - 1, 0)
                 q_turn(it - 1, 1)
-            if ok(it + 3) and it < 2:
-                w_scale(it + 3, (0,))
-            if ok(it):
-                h1(it)
-            if ok(it - 2):
-                fin(it - 2, 1)
-                stores(it - 2)
-            if ok(it + 3) and it < 2:
-                w_scale(it + 3, (1,))
-            if ok(it):
-                h2(it)
-            if ok(it + 1):
-                ring(it + 1)
-                mx_kv(it + 1, 0)
-                mx_kv(it + 1, 1)
-            if ok(it):
-                mx_q(it, 0)
-                mx_q(it, 1)
-                q_bias(it, 0)
-                q_bias(it, 1)
-            if ok(it - 1):
                 vertical(it - 1, 0)
                 vertical(it - 1, 1)
             if ok(it):
-                neighbours(it, 0)
-                neighbours(it, 1)
-            if ok(it + 3):
-                w_scale(it + 3, (2,) if it < 2 else (0, 1, 2))
+                h2(it)
             if ok(it + 2):
-                w_quant(it + 2)
+                w_quant(it + 2, (0,))
+            if ok(it + 1):
+                kv_mul(it + 1, 0)
+            if ok(it + 2):
+                w_quant(it + 2, (1,))
+            if ok(it + 4):
+                w_scale(it + 4, (0,))
             if ok(it) and it >= LATE:
                 upper_tap(it)
+            if ok(it + 1):
+                kv_mul(it + 1, 1)
+            if ok(it + 4):
+                w_scale(it + 4, (1,))
+            if ok(it - 1):
+                fin(it - 1, 0)
+            if ok(it + 1):
+                h1(it + 1)
+            if ok(it + 4):
+                w_scale(it + 4, (2,))
+            if ok(it - 1):
+                fin(it - 1, 1)
+                stores(it - 1)
+            if ok(it):
+                neighbours(it, 0)
+                neighbours(it, 1)
+            if ok(it + 1):
+                mx_q(it + 1, 0)
+                mx_q(it + 1, 1)
+                q_bias(it + 1, 0)
+                q_bias(it + 1, 1)
+            if ok(it + 2):
+                mx_kv(it + 2, 0)
+                mx_kv(it + 2, 1)
+            if ok(it + 3):
+                w_turn(it + 3)

@@ -17,7 +17,7 @@ FLOPS = 2 * 1024 * 1024 * 3072
 
 P = 128
 NT = 8
-LATE = 6
+LATE = 5
 
 
 def tile_attentionconv_kernel(tc, x, W_qkv_bytes, W_qkv_scale, b_qkv, out):
@@ -72,9 +72,7 @@ def tile_attentionconv_kernel(tc, x, W_qkv_bytes, W_qkv_scale, b_qkv, out):
                     )
 
         load_scale_rows()
-        load_w_rows(0, slice(0, 1))
-        load_scale_bc()
-        load_w_rows(0, slice(1, 3))
+        load_w(0)
         load_w(1)
         load_x(0, 0)
         load_bias()
@@ -115,7 +113,7 @@ def tile_attentionconv_kernel(tc, x, W_qkv_bytes, W_qkv_scale, b_qkv, out):
         sps = ps.tile([P, P], F32, name="sps", tag="ev", bufs=4)
         nc.tensor.transpose(out=sps[:], in_=srow[:], identity=ident[:])
         nc.vector.tensor_copy(out=scol[:], in_=sps[:, 0:8])
-        for h in range(512 // 512, 2):
+        for h in range(0, 2):
             spb = ps.tile([P, 4, P], F32, name="spb", tag="ev", bufs=4)
             for q4 in range(4):
                 m = 4 * h + q4
@@ -199,21 +197,23 @@ def tile_attentionconv_kernel(tc, x, W_qkv_bytes, W_qkv_scale, b_qkv, out):
                 xs[(g, n)] = xpool.tile([P, 512], U8, name="xs%d%d" % (g, n), tag="xs%d%d" % (g, n), align_bytes=64)
 
         def x_reorder(n, c, engines="ss"):
-            xr_v = xr[n][:].rearrange("p (jl u c r s4) -> p u c jl r s4", jl=8, u=2, c=2, r=16)
-            xw = xin[(n, c)][:].bitcast(F32).rearrange("p (r jl s4 u) -> p u jl r s4", r=16, jl=8, s4=4)
-            for u in range(2):
-                if engines[u] == "v":
-                    nc.vector.tensor_copy(out=xr_v[:, u, c], in_=xw[:, u])
-                elif engines[u] == "s":
-                    nc.scalar.copy(out=xr_v[:, u, c], in_=xw[:, u])
+            xr_v = xr[n][:].rearrange("p (h jl c r s) -> p h c jl r s", h=2, jl=4, c=2, r=16)
+            xw = xin[(n, c)][:].bitcast(F32).rearrange("p (r h jl s) -> p h jl r s", r=16, h=2, jl=4)
+            for h in range(2):
+                if engines[h] == "v":
+                    nc.vector.tensor_copy(out=xr_v[:, h, c], in_=xw[:, h])
+                elif engines[h] == "s":
+                    nc.scalar.copy(out=xr_v[:, h, c], in_=xw[:, h])
 
         def x_turn(n, parts=(0, 1, 2, 3)):
             xg_v = xg[n][:].bitcast(F32).rearrange("p g (a jl m u) -> p a g jl m u", a=4, jl=2, u=2)
             for a in parts:
                 trp = ps.tile([P, 4, P], F32, name="trp", tag="ev", bufs=4)
                 for q4 in range(4):
-                    nc.tensor.transpose(out=trp[:, q4, :], in_=xr[n][:, P * (4 * a + q4) : P * (4 * a + q4 + 1)], identity=ident[:])
-                nc.scalar.copy(out=xg_v[:, a], in_=trp[:].rearrange("p (jl u) (g m) -> p g jl m u", u=2, g=2))
+                    first = 256 * (2 * a + q4 // 2) + q4 % 2
+                    nc.tensor.transpose(out=trp[:, q4, :], in_=xr[n][:, first : first + 255 : 2], identity=ident[:])
+                for g in range(2):
+                    nc.scalar.copy(out=xg_v[:, a, g], in_=trp[:].rearrange("p (jl u) (g m) -> p g jl m u", u=2, g=2)[:, g])
 
         def x_quant(n, g):
             nc.vector.quantize_mx(out=xq[(g, n)][:].bitcast(FP8X4), scales=xs[(g, n)][:], in_=xg[n][:, g, :])
@@ -245,9 +245,10 @@ def tile_attentionconv_kernel(tc, x, W_qkv_bytes, W_qkv_scale, b_qkv, out):
             nc.scalar.activation(out=dst, in_=src, func=ACT.Identity, bias=col, scale=1.0)
 
         def ring(t):
-            kvp = epi.tile([P, 18, 64], F32, name="kvp", tag="kvp", bufs=3)
-            fill(kvp[:, 0:18:17, :], zeros[:].rearrange("p (a c) -> p a c", c=64), bkbv[:, t : t + 1])
-            kvp_of[t] = kvp
+            kvp_of[t] = epi.tile([P, 18, 64], F32, name="kvp", tag="kvp", bufs=3)
+            fill(kvp_of[t][:, 0:18:17, :], zeros[:].rearrange("p (a c) -> p a c", c=64), bkbv[:, t : t + 1])
+
+        def uring(t):
             zb = zeros[:, 0:64].rearrange("p (a c) -> p a c", c=4)
             u2_of[t] = epi.tile([P, 16, 64], F32, name="u2", tag="u2", bufs=3)
             fill(u2_of[t][:, :, 60:64], zb, ub2[:, t : t + 1])
@@ -382,6 +383,7 @@ def tile_attentionconv_kernel(tc, x, W_qkv_bytes, W_qkv_scale, b_qkv, out):
         x_quant(0, 1)
         bias4()
         ring(0)
+        uring(0)
         mx_kv(0, 0)
         x_reorder(1, 0, "vv")
         x_reorder(1, 1, "vv")
@@ -408,6 +410,7 @@ def tile_attentionconv_kernel(tc, x, W_qkv_bytes, W_qkv_scale, b_qkv, out):
         for it in range(0, NT + 2):
             if ok(it + 1):
                 ring(it + 1)
+                uring(it + 1)
             if ok(it - 1):
                 q_turn(it - 1, 0)
                 q_turn(it - 1, 1)
@@ -415,10 +418,10 @@ def tile_attentionconv_kernel(tc, x, W_qkv_bytes, W_qkv_scale, b_qkv, out):
                 vertical(it - 1, 1)
             if ok(it):
                 h2(it)
-            if ok(it + 2):
-                w_quant(it + 2, (0,))
             if ok(it + 1):
                 kv_mul(it + 1, 0)
+            if ok(it + 2):
+                w_quant(it + 2, (0,))
             if ok(it + 2):
                 w_quant(it + 2, (1,))
             if ok(it + 4):

@@ -62,15 +62,20 @@ def tile_attentionconv_kernel(tc, x, W_qkv_bytes, W_qkv_scale, b_qkv, out):
                 wbytes[t] = wkeep.tile([P, 3, 1024], U8, name="wbytes%d" % t, tag="wbytes%d" % t)
             nc.sync.dma_start(out=wbytes[t][:, js, :], in_=w_rows[:, t : 24 : NT, :][:, js, :])
 
-        def load_x(n, c, queue=nc.sync):
-            xin[(n, c)] = xpool.tile([P, 2048], BF16, name="xin%d%d" % (n, c), tag="xin%d%d" % (n, c))
-            for b in range(4):
+        def load_x(n, c, queue=nc.sync, bs=(0, 1, 2, 3)):
+            if (n, c) not in xin:
+                xin[(n, c)] = xpool.tile([P, 2048], BF16, name="xin%d%d" % (n, c), tag="xin%d%d" % (n, c))
+            for b in bs:
                 for g in range(2):
                     queue.dma_start(
                         out=xin[(n, c)][64 * g + b : 64 * (g + 1) : 4, :].rearrange("p (r w) -> p r w", r=16),
                         in_=x[b, 2 * g + c].rearrange("(i r) (jh w) -> jh i r w", r=16, jh=2)[n],
                     )
 
+        ident = const.tile([P, P], F32, name="ident", tag="ident")
+        make_identity(nc, ident[:])
+        identb = const.tile([P, P], BF16, name="identb", tag="identb")
+        make_identity(nc, identb[:])
         load_scale_rows()
         load_w(0)
         load_w(1)
@@ -79,15 +84,12 @@ def tile_attentionconv_kernel(tc, x, W_qkv_bytes, W_qkv_scale, b_qkv, out):
         load_x(0, 1)
         load_w(2)
         load_x(1, 0)
-        load_x(1, 1)
+        load_x(1, 1, bs=(0, 1, 2))
         load_w(3)
         for t in range(4, NT):
             load_w(t)
+        load_x(1, 1, nc.gpsimd, (3,))
 
-        ident = const.tile([P, P], F32, name="ident", tag="ident")
-        make_identity(nc, ident[:])
-        identb = const.tile([P, P], BF16, name="identb", tag="identb")
-        make_identity(nc, identb[:])
         zeros = const.tile([P, P], F32, name="zeros", tag="zeros")
         nc.vector.memset(zeros[:], 0.0)
 
@@ -113,14 +115,11 @@ def tile_attentionconv_kernel(tc, x, W_qkv_bytes, W_qkv_scale, b_qkv, out):
         sps = ps.tile([P, P], F32, name="sps", tag="ev", bufs=4)
         nc.tensor.transpose(out=sps[:], in_=srow[:], identity=ident[:])
         nc.vector.tensor_copy(out=scol[:], in_=sps[:, 0:8])
-        for h in range(0, 2):
-            spb = ps.tile([P, 4, P], F32, name="spb", tag="ev", bufs=4)
-            for q4 in range(4):
-                m = 4 * h + q4
-                nc.tensor.transpose(out=spb[:, q4, :], in_=scol[:, m : m + 1].to_broadcast([P, P]), identity=ident[:])
-            (nc.vector.tensor_copy if h == 0 else nc.scalar.copy)(
-                out=scale_bc[:, 512 * h : 512 * (h + 1)], in_=spb[:].rearrange("p q n -> p (q n)")
-            )
+        for first, blocks, copy in ((0, 2, nc.vector.tensor_copy), (2, 2, nc.scalar.copy), (4, 4, nc.scalar.copy)):
+            spb = ps.tile([P, blocks, P], F32, name="spb", tag="ev", bufs=4)
+            for m in range(blocks):
+                nc.tensor.transpose(out=spb[:, m, :], in_=scol[:, first + m : first + m + 1].to_broadcast([P, P]), identity=ident[:])
+            copy(out=scale_bc[:, P * first : P * (first + blocks)], in_=spb[:].rearrange("p m n -> p (m n)"))
 
         csum = const.tile([P, 1], F32, name="csum", tag="csum")
         nc.vector.scalar_tensor_tensor(out=csum[:], in0=c0, scalar=1.0, in1=c2, op0=ALU.add, op1=ALU.add)
@@ -154,10 +153,9 @@ def tile_attentionconv_kernel(tc, x, W_qkv_bytes, W_qkv_scale, b_qkv, out):
         wq = {}
         ws = {}
 
-        def w_scale(t, js=(0, 1, 2), hs=(0, 1)):
+        def w_scale(t, js=(0, 1, 2), ks=slice(0, 1024)):
             if t not in wsc_of:
                 wsc_of[t] = wwork.tile([P, 3, 1024], BF16, name="wsc", tag="wsc", bufs=3)
-            ks = slice(512 * hs[0], 512 * (hs[-1] + 1))
             for j in js:
                 nc.vector.tensor_tensor(out=wsc_of[t][:, j, ks], in0=wbytes[t][:, j, ks].bitcast(FP8), in1=scale_bc[:, ks], op=ALU.mult)
 
@@ -329,7 +327,7 @@ def tile_attentionconv_kernel(tc, x, W_qkv_bytes, W_qkv_scale, b_qkv, out):
 
         def vertical(t, h):
             terms = ([tt_of[t][:]] if t < LATE else []) + [u_of[t][:].rearrange("p k c -> p (k c)") for u_of in (u0_of, u2_of)]
-            stp = ps.tile([P, 4, P], F32, name="stp", tag="sT", bufs=2)
+            stp = ps.tile([P, 4, P], F32, name="stp", tag="ev", bufs=4) if t == NT - 1 else ps.tile([P, 4, P], F32, name="stp", tag="sT", bufs=2)
             for q4 in range(4):
                 for i, term in enumerate(terms):
                     nc.tensor.matmul(
@@ -361,8 +359,9 @@ def tile_attentionconv_kernel(tc, x, W_qkv_bytes, W_qkv_scale, b_qkv, out):
         def ok(t):
             return 0 <= t < NT
 
-        w_scale(0, hs=(0,))
-        w_scale(0, hs=(1,))
+        w_scale(0, ks=slice(0, 256))
+        w_scale(0, ks=slice(256, 512))
+        w_scale(0, ks=slice(512, 1024))
         w_turn(0)
         x_reorder(0, 0, "ss")
         w_scale(1, (0,))
@@ -370,12 +369,12 @@ def tile_attentionconv_kernel(tc, x, W_qkv_bytes, W_qkv_scale, b_qkv, out):
         w_scale(1, (2,))
         w_turn(1, (0, 1))
         x_reorder(0, 1, "vv")
-        x_turn(0)
         bias_turn()
+        bias1()
+        x_turn(0)
         w_turn(1, (2,))
         w_quant(0)
         w_scale(2, (0,))
-        bias1()
         w_scale(2, (1,))
         bias2()
         x_quant(0, 0)
@@ -386,7 +385,7 @@ def tile_attentionconv_kernel(tc, x, W_qkv_bytes, W_qkv_scale, b_qkv, out):
         uring(0)
         mx_kv(0, 0)
         x_reorder(1, 0, "vv")
-        x_reorder(1, 1, "vv")
+        x_reorder(1, 1, "vs")
         x_turn(1)
         w_quant(1)
         w_scale(2, (2,))
@@ -403,9 +402,11 @@ def tile_attentionconv_kernel(tc, x, W_qkv_bytes, W_qkv_scale, b_qkv, out):
         w_scale(3, (1,))
         w_scale(3, (2,))
         kv_mul(0, 1)
+        w_quant(2, (0,))
         mx_kv(1, 0)
         mx_kv(1, 1)
         h1(0)
+        w_quant(2, (1,))
 
         for it in range(0, NT + 2):
             if ok(it + 1):
@@ -420,14 +421,14 @@ def tile_attentionconv_kernel(tc, x, W_qkv_bytes, W_qkv_scale, b_qkv, out):
                 h2(it)
             if ok(it + 1):
                 kv_mul(it + 1, 0)
-            if ok(it + 2):
+            if ok(it + 2) and it > 0:
                 w_quant(it + 2, (0,))
-            if ok(it + 2):
+            if ok(it + 2) and it > 0:
                 w_quant(it + 2, (1,))
             if ok(it + 4):
                 w_scale(it + 4, (0,))
             if ok(it) and it >= LATE:
-                upper_tap(it)
+                upper_tap(it, slice(0, 8) if it == NT - 1 else slice(0, 16))
             if ok(it + 1):
                 kv_mul(it + 1, 1)
             if ok(it + 4):
@@ -441,6 +442,8 @@ def tile_attentionconv_kernel(tc, x, W_qkv_bytes, W_qkv_scale, b_qkv, out):
             if ok(it - 1):
                 fin(it - 1, 1)
                 stores(it - 1)
+            if it == NT - 1:
+                upper_tap(it, slice(8, 16))
             if ok(it):
                 neighbours(it, 0)
                 neighbours(it, 1)

@@ -31,10 +31,10 @@ def tile_attentionconv_kernel(tc, x, W_qkv_bytes, W_qkv_scale, b_qkv, out):
         ps = ctx.enter_context(tc.psum_pool(name="ps", bufs=2))
         ctx.enter_context(tc.manual_schedule())
 
+        srow = const.tile([P, P], F32, name="srow", tag="srow")
+        nc.gpsimd.memset(srow[:], 0.0)
         pidx = const.tile([P, 1], I32, name="pidx", tag="pidx")
         nc.gpsimd.iota(pidx[:], pattern=[[0, 1]], base=0, channel_multiplier=1)
-        srow = const.tile([P, P], F32, name="srow", tag="srow")
-        nc.vector.memset(srow[:], 0.0)
         brow = const.tile([P, P], BF16, name="brow", tag="brow")
         nc.gpsimd.memset(brow[:], 0.0)
         b_rows = b_qkv.rearrange("(w m) -> w m", m=P)
@@ -368,7 +368,7 @@ def tile_attentionconv_kernel(tc, x, W_qkv_bytes, W_qkv_scale, b_qkv, out):
         w_scale(1, (1,))
         w_scale(1, (2,))
         w_turn(1, (0, 1))
-        x_reorder(0, 1, "vv")
+        x_reorder(0, 1, "vs")
         bias_turn()
         bias1()
         x_turn(0)

from contextlib import ExitStack

import concourse.mybir as mybir
from concourse.masks import make_identity

F32 = mybir.dt.float32
BF16 = mybir.dt.bfloat16
U8 = mybir.dt.uint8
U32 = mybir.dt.uint32
I32 = mybir.dt.int32
FP8 = mybir.dt.float8_e4m3fn
FP8X4 = mybir.dt.float8_e4m3fn_x4
ALU = mybir.AluOpType
ACT = mybir.ActivationFunctionType

FLOPS = 2 * 1024 * 1024 * 3072

P = 128
NT = 8
LATE = 5


def tile_attentionconv_kernel(tc, x, W_qkv_bytes, W_qkv_scale, b_qkv, out):
    nc = tc.nc
    with ExitStack() as ctx:
        const = ctx.enter_context(tc.tile_pool(name="const", bufs=1))
        xpool = ctx.enter_context(tc.tile_pool(name="xpool", bufs=1))
        wkeep = ctx.enter_context(tc.tile_pool(name="wkeep", bufs=1))
        wwork = ctx.enter_context(tc.tile_pool(name="wwork", bufs=2))
        epi = ctx.enter_context(tc.tile_pool(name="epi", bufs=2))
        ps = ctx.enter_context(tc.psum_pool(name="ps", bufs=2))
        ctx.enter_context(tc.manual_schedule())

        srow = const.tile([P, P], F32, name="srow", tag="srow")
        nc.gpsimd.memset(srow[:], 0.0)
        pidx = const.tile([P, 1], I32, name="pidx", tag="pidx")
        nc.gpsimd.iota(pidx[:], pattern=[[0, 1]], base=0, channel_multiplier=1)
        brow = const.tile([P, P], BF16, name="brow", tag="brow")
        nc.gpsimd.memset(brow[:], 0.0)
        b_rows = b_qkv.rearrange("(w m) -> w m", m=P)
        scale_bc = const.tile([P, 1024], F32, name="scale_bc", tag="scale_bc")
        w_rows = W_qkv_bytes.rearrange("(w m) k -> m w k", m=P)
        wbytes = {}
        xin = {}

        def load_scale_rows():
            nc.sync.dma_start(out=srow[0:8, :], in_=W_qkv_scale.rearrange("o (m n) -> (o m) n", n=P))

        def load_scale_bc():
            nc.sync.dma_start(out=scale_bc[:, 0:512], in_=W_qkv_scale.rearrange("o k -> (o k)")[0:512].partition_broadcast(P))

        def load_bias():
            nc.sync.dma_start(out=brow[0:16, :], in_=b_rows[0:16, :])
            nc.sync.dma_start(out=brow[16:24, :], in_=b_rows[16:24, :])

        def load_w(t):
            wbytes[t] = wkeep.tile([P, 3, 1024], U8, name="wbytes%d" % t, tag="wbytes%d" % t)
            nc.sync.dma_start(out=wbytes[t][:], in_=w_rows[:, t : 24 : NT, :])

        def load_w_rows(t, js):
            if t not in wbytes:
                wbytes[t] = wkeep.tile([P, 3, 1024], U8, name="wbytes%d" % t, tag="wbytes%d" % t)
            nc.sync.dma_start(out=wbytes[t][:, js, :], in_=w_rows[:, t : 24 : NT, :][:, js, :])

        def load_x(n, c, queue=nc.sync, bs=(0, 1, 2, 3)):
            if (n, c) not in xin:
                xin[(n, c)] = xpool.tile([P, 2048], BF16, name="xin%d%d" % (n, c), tag="xin%d%d" % (n, c))
            for b in bs:
                for g in range(2):
                    queue.dma_start(
                        out=xin[(n, c)][64 * g + b : 64 * (g + 1) : 4, :].rearrange("p (r w) -> p r w", r=16),
                        in_=x[b, 2 * g + c].rearrange("(i r) (jh w) -> jh i r w", r=16, jh=2)[n],
                    )

        ident = const.tile([P, P], F32, name="ident", tag="ident")
        make_identity(nc, ident[:])
        identb = const.tile([P, P], BF16, name="identb", tag="identb")
        make_identity(nc, identb[:])
        load_scale_rows()
        load_w(0)
        load_w(1)
        load_x(0, 0)
        load_bias()
        load_x(0, 1)
        load_w(2)
        load_x(1, 0)
        load_x(1, 1, bs=(0, 1, 2))
        load_w(3)
        for t in range(4, NT):
            load_w(t)
        load_x(1, 1, nc.gpsimd, (3,))

        zeros = const.tile([P, P], F32, name="zeros", tag="zeros")
        nc.vector.memset(zeros[:], 0.0)

        sr_i = const.tile([P, 2], I32, name="sr_i", tag="sr_i")
        nc.vector.tensor_scalar(out=sr_i[:, 0:1], in0=pidx[:], scalar1=15, scalar2=None, op0=ALU.bitwise_and)
        nc.vector.tensor_scalar(out=sr_i[:, 1:2], in0=pidx[:], scalar1=4, scalar2=None, op0=ALU.logical_shift_right)
        sr_f = const.tile([P, 2], F32, name="sr_f", tag="sr_f")
        nc.vector.tensor_copy(out=sr_f[:], in_=sr_i[:])
        args = const.tile([P, 6], F32, name="args", tag="args")
        for col, (src_col, mul, add) in enumerate(
            [(0, 0.125, -1.875), (0, -0.125, 0.0), (1, 0.125, -1.875), (1, 0.125, -0.875), (1, -0.125, 0.0), (1, -0.125, -1.0)]
        ):
            nc.vector.tensor_scalar(
                out=args[:, col : col + 1], in0=sr_f[:, src_col : src_col + 1],
                scalar1=mul, scalar2=add, op0=ALU.mult, op1=ALU.add,
            )
        cf = const.tile([P, 6], F32, name="cf", tag="cf")
        nc.scalar.activation(out=cf[:], in_=args[:], func=ACT.Exp)
        c0 = cf[:, 0:1]
        c2 = cf[:, 1:2]

        scol = const.tile([P, 8], F32, name="scol", tag="scol")
        sps = ps.tile([P, P], F32, name="sps", tag="ev", bufs=4)
        nc.tensor.transpose(out=sps[:], in_=srow[:], identity=ident[:])
        nc.vector.tensor_copy(out=scol[:], in_=sps[:, 0:8])
        for first, blocks, copy in ((0, 2, nc.vector.tensor_copy), (2, 2, nc.scalar.copy), (4, 4, nc.scalar.copy)):
            spb = ps.tile([P, blocks, P], F32, name="spb", tag="ev", bufs=4)
            for m in range(blocks):
                nc.tensor.transpose(out=spb[:, m, :], in_=scol[:, first + m : first + m + 1].to_broadcast([P, P]), identity=ident[:])
            copy(out=scale_bc[:, P * first : P * (first + blocks)], in_=spb[:].rearrange("p m n -> p (m n)"))

        csum = const.tile([P, 1], F32, name="csum", tag="csum")
        nc.vector.scalar_tensor_tensor(out=csum[:], in0=c0, scalar=1.0, in1=c2, op0=ALU.add, op1=ALU.add)
        b_f = const.tile([P, 24], F32, name="b_f", tag="b_f")
        bkbv = const.tile([P, NT], F32, name="bkbv", tag="bkbv")
        tbord = const.tile([P, NT], F32, name="tbord", tag="tbord")
        ub0 = const.tile([P, NT], F32, name="ub0", tag="ub0")
        ub2 = const.tile([P, NT], F32, name="ub2", tag="ub2")
        bps_of = {}

        def bias_turn():
            bps_of[0] = ps.tile([P, P], BF16, name="bps", tag="ev", bufs=4)
            nc.tensor.transpose(out=bps_of[0][:], in_=brow[:], identity=identb[:])

        def bias1():
            nc.vector.tensor_copy(out=b_f[:], in_=bps_of[0][:, 0:24])

        def bias2():
            nc.vector.tensor_tensor(out=bkbv[:], in0=b_f[:, 8:16], in1=b_f[:, 16:24], op=ALU.mult)

        def bias3():
            nc.vector.tensor_scalar(out=tbord[:], in0=bkbv[:], scalar1=csum[:], scalar2=None, op0=ALU.mult)

        def bias4():
            for rh in range(2):
                nc.vector.tensor_scalar(out=ub0[:, rh:NT:2], in0=tbord[:, rh:NT:2], scalar1=cf[:, 2 + rh : 3 + rh], scalar2=None, op0=ALU.mult)
                nc.vector.tensor_scalar(out=ub2[:, rh:NT:2], in0=tbord[:, rh:NT:2], scalar1=cf[:, 4 + rh : 5 + rh], scalar2=None, op0=ALU.mult)

        wsc_of = {}
        wg_of = {}
        wq = {}
        ws = {}

        def w_scale(t, js=(0, 1, 2), ks=slice(0, 1024)):
            if t not in wsc_of:
                wsc_of[t] = wwork.tile([P, 3, 1024], BF16, name="wsc", tag="wsc", bufs=3)
            for j in js:
                nc.vector.tensor_tensor(out=wsc_of[t][:, j, ks], in0=wbytes[t][:, j, ks].bitcast(FP8), in1=scale_bc[:, ks], op=ALU.mult)

        def w_turn(t, js=(0, 1, 2)):
            if t not in wg_of:
                wg_of[t] = wwork.tile([P, 3072], BF16, name="wg", tag="wg", align_bytes=64, bufs=2)
            for j in js:
                words = wsc_of[t][:, j, :].bitcast(F32)
                trp = ps.tile([P, 4, P], F32, name="trp", tag="ev", bufs=4)
                for g in range(2):
                    for u in range(2):
                        nc.tensor.transpose(out=trp[:, 2 * g + u, :], in_=words[:, 256 * g + u : 256 * (g + 1) : 2], identity=ident[:])
                nc.scalar.copy(
                    out=wg_of[t][:, 1024 * j : 1024 * (j + 1)].bitcast(F32).rearrange("p (g m u) -> p g m u", g=2, u=2),
                    in_=trp[:].rearrange("p (g u) m -> p g m u", g=2),
                )

        def w_quant(t, part=(0, 1)):
            if t not in wq:
                wq[t] = wkeep.tile([P, 768], U32, name="wq%d" % t, tag="wq%d" % t, align_bytes=64)
                ws[t] = wkeep.tile([P, 768], U8, name="ws%d" % t, tag="ws%d" % t, align_bytes=64)
            for i in part:
                cols = slice(0, 512) if i == 0 else slice(512, 768)
                nc.vector.quantize_mx(
                    out=wq[t][:, cols].bitcast(FP8X4), scales=ws[t][:, cols], in_=wg_of[t][:, 4 * cols.start : 4 * cols.stop]
                )

        xr = {}
        xg = {}
        xq = {}
        xs = {}
        for n in range(2):
            xr[n] = xpool.tile([P, 2048], F32, name="xr%d" % n, tag="xr%d" % n)
            xg[n] = xpool.tile([P, 2, 2048], BF16, name="xg%d" % n, tag="xg%d" % n, align_bytes=64)
            for g in range(2):
                xq[(g, n)] = xpool.tile([P, 512], U32, name="xq%d%d" % (g, n), tag="xq%d%d" % (g, n), align_bytes=64)
                xs[(g, n)] = xpool.tile([P, 512], U8, name="xs%d%d" % (g, n), tag="xs%d%d" % (g, n), align_bytes=64)

        def x_reorder(n, c, engines="ss"):
            xr_v = xr[n][:].rearrange("p (h jl c r s) -> p h c jl r s", h=2, jl=4, c=2, r=16)
            xw = xin[(n, c)][:].bitcast(F32).rearrange("p (r h jl s) -> p h jl r s", r=16, h=2, jl=4)
            for h in range(2):
                if engines[h] == "v":
                    nc.vector.tensor_copy(out=xr_v[:, h, c], in_=xw[:, h])
                elif engines[h] == "s":
                    nc.scalar.copy(out=xr_v[:, h, c], in_=xw[:, h])

        def x_turn(n, parts=(0, 1, 2, 3)):
            xg_v = xg[n][:].bitcast(F32).rearrange("p g (a jl m u) -> p a g jl m u", a=4, jl=2, u=2)
            for a in parts:
                trp = ps.tile([P, 4, P], F32, name="trp", tag="ev", bufs=4)
                for q4 in range(4):
                    first = 256 * (2 * a + q4 // 2) + q4 % 2
                    nc.tensor.transpose(out=trp[:, q4, :], in_=xr[n][:, first : first + 255 : 2], identity=ident[:])
                for g in range(2):
                    nc.scalar.copy(out=xg_v[:, a, g], in_=trp[:].rearrange("p (jl u) (g m) -> p g jl m u", u=2, g=2)[:, g])

        def x_quant(n, g):
            nc.vector.quantize_mx(out=xq[(g, n)][:].bitcast(FP8X4), scales=xs[(g, n)][:], in_=xg[n][:, g, :])

        def project(t, j, n, tag):
            acc = ps.tile([P, 512], F32, name="acc_" + tag, tag=tag, bufs=(4 if tag == "ev" else 2))
            for g in range(2):
                cols = slice(256 * j + P * g, 256 * j + P * (g + 1))
                nc.tensor.matmul_mx(
                    out=acc[:], lhsT=wq[t][:, cols].bitcast(FP8X4), lhsT_scale=ws[t][:, cols],
                    rhs=xq[(g, n)][:].bitcast(FP8X4), rhs_scale=xs[(g, n)][:], start=(g == 0), stop=(g == 1),
                )
            return acc

        kvp_of = {}
        tmp_of = {}
        tt_of = {}
        u0_of = {}
        u2_of = {}
        kp_of = {}
        vacc_of = {}
        qacc_of = {}
        qp_of = {}
        qts_of = {}
        stp_of = {}
        ot_of = {}

        def fill(dst, src, col):
            nc.scalar.activation(out=dst, in_=src, func=ACT.Identity, bias=col, scale=1.0)

        def ring(t):
            kvp_of[t] = epi.tile([P, 18, 64], F32, name="kvp", tag="kvp", bufs=3)
            fill(kvp_of[t][:, 0:18:17, :], zeros[:].rearrange("p (a c) -> p a c", c=64), bkbv[:, t : t + 1])

        def uring(t):
            zb = zeros[:, 0:64].rearrange("p (a c) -> p a c", c=4)
            u2_of[t] = epi.tile([P, 16, 64], F32, name="u2", tag="u2", bufs=3)
            fill(u2_of[t][:, :, 60:64], zb, ub2[:, t : t + 1])
            u0_of[t] = epi.tile([P, 16, 64], F32, name="u0", tag="u0", bufs=3)
            if t < LATE:
                fill(u0_of[t][:, :, 0:4], zb, ub0[:, t : t + 1])

        def mx_kv(t, n):
            kacc = project(t, 1, n, "ev")
            vacc_of[(t, n)] = project(t, 2, n, "v")
            kp = epi.tile([P, 512], F32, name="kp", tag="kp", bufs=4)
            nc.scalar.activation(out=kp[:], in_=kacc[:], func=ACT.Identity, bias=b_f[:, 8 + t : 9 + t], scale=1.0)
            kp_of[(t, n)] = kp

        def mx_q(t, n):
            qacc_of[(t, n)] = project(t, 0, n, "ev")

        def q_bias(t, n):
            if t not in qp_of:
                qp_of[t] = epi.tile([P, 8, 2, 64], F32, name="qp", tag="qp", bufs=2)
            nc.scalar.activation(
                out=qp_of[t][:, :, n, :], in_=qacc_of[(t, n)][:].rearrange("p (jl m) -> p jl m", m=64), func=ACT.Identity, bias=b_f[:, t : t + 1], scale=1.0
            )

        def kv_mul(t, n):
            nc.vector.scalar_tensor_tensor(
                out=kvp_of[t][:, 1 + n : 17 : 2, :], in0=vacc_of[(t, n)][:].rearrange("p (jl m) -> p jl m", m=64), scalar=b_f[:, 16 + t : 17 + t],
                in1=kp_of[(t, n)][:].rearrange("p (jl m) -> p jl m", m=64), op0=ALU.add, op1=ALU.mult,
            )

        def q_turn(t, h):
            qp = qp_of[t][:].rearrange("p jl n m -> p (jl n m)")
            qtp = ps.tile([P, 4, P], F32, name="qtp", tag="ev", bufs=4)
            for q4 in range(4):
                nc.tensor.transpose(out=qtp[:, q4, :], in_=qp[:, P * (4 * h + q4) : P * (4 * h + q4 + 1)], identity=ident[:])
            qts = epi.tile([P, 512], F32, name="qts", tag="qts", bufs=4)
            nc.scalar.copy(out=qts[:], in_=qtp[:].rearrange("p jl e -> p (jl e)"))
            qts_of[(t, h)] = qts

        def h1(t):
            kvp = kvp_of[t]
            kvf = kvp[:].rearrange("p k m -> p (k m)")
            tmp = epi.tile([P, 1024], F32, name="tmp", tag="tmp", bufs=1)
            nc.vector.scalar_tensor_tensor(out=tmp[:, 128:1024], in0=kvf[:, 64:960], scalar=c0, in1=kvf[:, 192:1088], op0=ALU.mult, op1=ALU.add)
            nc.vector.scalar_tensor_tensor(
                out=tmp[:, 0:128].rearrange("p (k c) -> p k c", c=64), in0=kvp[:, 0:16:15, :], scalar=c0, in1=kvp[:, 1:3, :],
                op0=ALU.mult, op1=ALU.add,
            )
            tmp_of[t] = tmp

        def h2(t):
            kvp = kvp_of[t]
            kvf = kvp[:].rearrange("p k m -> p (k m)")
            tmp = tmp_of[t]
            tt = epi.tile([P, 1024], F32, name="tt", tag="tt", bufs=3)
            nc.vector.scalar_tensor_tensor(out=tt[:, 0:896], in0=kvf[:, 192:1088], scalar=c2, in1=tmp[:, 0:896], op0=ALU.mult, op1=ALU.add)
            nc.vector.scalar_tensor_tensor(
                out=tt[:, 896:1024].rearrange("p (k c) -> p k c", c=64), in0=kvp[:, 2:18:15, :], scalar=c2,
                in1=tmp[:, 896:1024].rearrange("p (k c) -> p k c", c=64), op0=ALU.mult, op1=ALU.add,
            )
            tt_of[t] = tt

        def upper_tap(t, ks=slice(0, 16)):
            rh = t % 2
            tv = tt_of[t][:].rearrange("p (k c) -> p k c", c=64)
            nc.vector.scalar_tensor_tensor(
                out=u0_of[t][:, ks, 4:64], in0=tv[:, ks, 0:60], scalar=cf[:, 2 + rh : 3 + rh], in1=tv[:, ks, 4:64], op0=ALU.mult, op1=ALU.add,
            )
            nc.vector.tensor_scalar(out=u0_of[t][:, ks, 0:4], in0=tv[:, ks, 0:4], scalar1=ub0[:, t : t + 1], scalar2=None, op0=ALU.add)

        def neighbours(t, h):
            rh = t % 2
            tv = tt_of[t][:].rearrange("p (k c) -> p k c", c=64)
            ks = slice(8 * h, 8 * (h + 1))
            if t < LATE:
                nc.scalar.activation(out=u0_of[t][:, ks, 4:64], in_=tv[:, ks, 0:60], func=ACT.Copy, scale=cf[:, 2 + rh : 3 + rh])
            nc.scalar.activation(out=u2_of[t][:, ks, 0:60], in_=tv[:, ks, 4:64], func=ACT.Copy, scale=cf[:, 4 + rh : 5 + rh])

        def vertical(t, h):
            terms = ([tt_of[t][:]] if t < LATE else []) + [u_of[t][:].rearrange("p k c -> p (k c)") for u_of in (u0_of, u2_of)]
            stp = ps.tile([P, 4, P], F32, name="stp", tag="ev", bufs=4) if t == NT - 1 else ps.tile([P, 4, P], F32, name="stp", tag="sT", bufs=2)
            for q4 in range(4):
                for i, term in enumerate(terms):
                    nc.tensor.matmul(
                        out=stp[:, q4, :], lhsT=term[:, P * (4 * h + q4) : P * (4 * h + q4 + 1)], rhs=ident[:],
                        start=(i == 0), stop=(i == len(terms) - 1), is_transpose=True,
                    )
            stp_of[(t, h)] = stp

        def fin(t, h):
            if h == 0:
                ot_of[t] = epi.tile([P, 1024], F32, name="ot", tag="ot", bufs=3)
            nc.vector.tensor_tensor(
                out=ot_of[t][:].rearrange("p (r jl s) -> p jl r s", r=8, jl=8)[:, 4 * h : 4 * (h + 1)],
                in0=stp_of[(t, h)][:].rearrange("p jl (r s) -> p jl r s", s=16),
                in1=qts_of[(t, h)][:].rearrange("p (jl r s) -> p jl r s", jl=4, s=16),
                op=ALU.mult,
            )

        def stores(t):
            ch, rh = divmod(t, 2)
            for b in range(4):
                dst = out[b, ch].rearrange("(i r) (jh w) -> jh i r w", r=16, jh=2)
                for jh in range(2):
                    nc.sync.dma_start(
                        out=dst[jh, :, 8 * rh : 8 * (rh + 1), :],
                        in_=ot_of[t][64 * jh + b : 64 * (jh + 1) : 4, :].rearrange("p (r w) -> p r w", r=8),
                    )

        def ok(t):
            return 0 <= t < NT

        w_scale(0, ks=slice(0, 256))
        w_scale(0, ks=slice(256, 512))
        w_scale(0, ks=slice(512, 1024))
        w_turn(0)
        x_reorder(0, 0, "ss")
        w_scale(1, (0,))
        w_scale(1, (1,))
        w_scale(1, (2,))
        w_turn(1, (0, 1))
        x_reorder(0, 1, "vs")
        bias_turn()
        bias1()
        x_turn(0)
        w_turn(1, (2,))
        w_quant(0)
        w_scale(2, (0,))
        w_scale(2, (1,))
        bias2()
        x_quant(0, 0)
        bias3()
        x_quant(0, 1)
        bias4()
        ring(0)
        uring(0)
        mx_kv(0, 0)
        x_reorder(1, 0, "vv")
        x_reorder(1, 1, "vs")
        x_turn(1)
        w_quant(1)
        w_scale(2, (2,))
        w_turn(2)
        w_scale(3, (0,))
        mx_q(0, 0)
        q_bias(0, 0)
        kv_mul(0, 0)
        x_quant(1, 0)
        x_quant(1, 1)
        mx_kv(0, 1)
        mx_q(0, 1)
        q_bias(0, 1)
        w_scale(3, (1,))
        w_scale(3, (2,))
        kv_mul(0, 1)
        w_quant(2, (0,))
        mx_kv(1, 0)
        mx_kv(1, 1)
        h1(0)
        w_quant(2, (1,))

        for it in range(0, NT + 2):
            if ok(it + 1):
                ring(it + 1)
                uring(it + 1)
            if ok(it - 1):
                q_turn(it - 1, 0)
                q_turn(it - 1, 1)
                vertical(it - 1, 0)
                vertical(it - 1, 1)
            if ok(it):
                h2(it)
            if ok(it + 1):
                kv_mul(it + 1, 0)
            if ok(it + 2) and it > 0:
                w_quant(it + 2, (0,))
            if ok(it + 2) and it > 0:
                w_quant(it + 2, (1,))
            if ok(it + 4):
                w_scale(it + 4, (0,))
            if ok(it) and it >= LATE:
                upper_tap(it, slice(0, 8) if it == NT - 1 else slice(0, 16))
            if ok(it + 1):
                kv_mul(it + 1, 1)
            if ok(it + 4):
                w_scale(it + 4, (1,))
            if ok(it - 1):
                fin(it - 1, 0)
            if ok(it + 1):
                h1(it + 1)
            if ok(it + 4):
                w_scale(it + 4, (2,))
            if ok(it - 1):
                fin(it - 1, 1)
                stores(it - 1)
            if it == NT - 1:
                upper_tap(it, slice(8, 16))
            if ok(it):
                neighbours(it, 0)
                neighbours(it, 1)
            if ok(it + 1):
                mx_q(it + 1, 0)
                mx_q(it + 1, 1)
                q_bias(it + 1, 0)
                q_bias(it + 1, 1)
            if ok(it + 2):
                mx_kv(it + 2, 0)
                mx_kv(it + 2, 1)
            if ok(it + 3):
                w_turn(it + 3)
